import numpy as np
import ml_dtypes


def mxq(x, axis, fmt="e4m3"):
    dtype, down = {"e4m3": (ml_dtypes.float8_e4m3fn, 7), "e5m2": (ml_dtypes.float8_e5m2, 14)}[fmt]
    v = np.moveaxis(np.asarray(x, np.float32).astype(ml_dtypes.bfloat16).astype(np.float64), axis, -1)
    blocks = v.reshape(v.shape[:-1] + (-1, 32))
    amax = np.abs(blocks).max(-1, keepdims=True)
    byte = np.maximum(np.where(amax > 0, np.frexp(amax)[1] - 1 + 127, 0) - down, 1)
    scale = np.exp2(byte - 127.0)
    codes = (blocks / scale).astype(np.float32).astype(dtype).astype(np.float64)
    return np.moveaxis((codes * scale).reshape(v.shape), -1, axis)


WIDE = False


def mx_kscale(k):
    if not WIDE:
        return np.ones(k)
    levels = np.array([10, -10, 5, -5, 0])
    a = np.random.permutation(np.resize(levels, k // 512 * 4)).reshape(k // 512, 4)
    idx = np.arange(k)
    return np.exp2(a[idx // 512, idx % 128 // 32])


BF16 = ml_dtypes.bfloat16


def bf(x):
    return np.asarray(x, np.float32).astype(BF16)


def f64(x):
    return np.asarray(x).astype(np.float64)


E2M1 = np.array([0.0, 0.5, 1.0, 1.5, 2.0, 3.0, 4.0, 6.0, -0.0, -0.5, -1.0, -1.5, -2.0, -3.0, -4.0, -6.0])


def pack_weight(w, fmt):
    k, n = w.shape
    w = f64(bf(w)).reshape(k // 32, 32, n)
    amax = np.abs(w).max(1)
    if fmt == "e4m3":
        byte = np.frexp(amax)[1] - 1 + 127 - 7
    else:
        mant, ex = np.frexp(amax / 6.0)
        byte = np.where(mant > 0.5, ex, ex - 1) + 127
    byte = np.clip(np.where(amax > 0, byte, 1), 1, 254)
    scaled = (w * np.exp2(127.0 - byte)[:, None, :]).reshape(k, n).astype(np.float32)
    by_word = np.ascontiguousarray(scaled.reshape(k // 512, 128, 4, n).transpose(0, 1, 3, 2))
    if fmt == "e4m3":
        words = by_word.astype(ml_dtypes.float8_e4m3fn).view(np.uint8)
    else:
        c = by_word.astype(ml_dtypes.float4_e2m1fn).view(np.uint8) & 0xF
        words = c[..., 0::2] | (c[..., 1::2] << 4)
    return np.ascontiguousarray(words), np.ascontiguousarray(byte.astype(np.uint8).reshape(k // 512, 16, n))


def unpack_weight(words, scales, fmt):
    g, p, n, _ = words.shape
    if fmt == "e4m3":
        vals = np.ascontiguousarray(words).view(ml_dtypes.float8_e4m3fn).astype(np.float64)
    else:
        nib = np.empty((g, p, n, 4), np.uint8)
        nib[..., 0::2] = words & 0xF
        nib[..., 1::2] = words >> 4
        vals = E2M1[nib]
    vals = vals * np.repeat(np.exp2(scales.astype(np.float64) - 127.0), 8, axis=1)[..., None]
    return vals.transpose(0, 1, 3, 2).reshape(g * 512, n)

def pack4(w):
    words, scales = pack_weight(w, "e2m1")
    return words.reshape(words.shape[0], 128, -1), scales


def unpack4(words, scales):
    return unpack_weight(words.reshape(words.shape[0], 128, -1, 2), scales, "e2m1")


B, S, C, HD = 1, 256, 1024, 128
H = C // HD
HP = HD // 2
EPS = 1e-6
THETA = 10000.0


def rmsnorm(h, g):
    return h * (1.0 / np.sqrt(np.mean(h * h, axis=-1, keepdims=True) + EPS)) * g


def apply_rope1(h, freqs):
    sh = h.shape
    h_ = h.reshape(*sh[:-1], -1, 1, 2)
    out = freqs[..., 0] * h_[..., 0] + freqs[..., 1] * h_[..., 1]
    return out.reshape(sh)


def setup_inputs():
    s = mx_kscale(C)
    pos = f64(np.random.randint(0, S, size=(S, 1)))
    inv_freq = 1.0 / THETA ** (np.arange(HP) / HP)
    ang = pos * inv_freq
    cos, sin = np.cos(ang), np.sin(ang)
    rot = np.stack([np.stack([cos, -sin], -1), np.stack([sin, cos], -1)], -2)
    x = bf(np.random.standard_normal((B, S, C)) * s)
    w = np.random.standard_normal((C, C)) / np.sqrt(C) / s[None, :]
    w_words, w_scales = pack4(np.ascontiguousarray(w.T))
    return {"x": x,
            "freqs": bf(rot[None, :, None]),
            "w_words": w_words,
            "w_scales": w_scales,
            "b": bf(np.random.standard_normal(C) * 0.3),
            "g": bf(1.0 + 0.1 * np.random.standard_normal(HD))}


def reference(x, freqs, w_words, w_scales, b, g):
    p = (mxq(f64(x), 2, "e4m3") @ unpack4(w_words, w_scales)) + f64(b)
    h = p.reshape(B, S, H, HD)
    return apply_rope1(rmsnorm(h, f64(g)), f64(freqs))

@@ -1,0 +1,220 @@
+from contextlib import ExitStack
+
+import concourse.mybir as mybir
+from concourse.masks import make_identity
+
+F32 = mybir.dt.float32
+BF16 = mybir.dt.bfloat16
+I32 = mybir.dt.int32
+U32 = mybir.dt.uint32
+U8 = mybir.dt.uint8
+FP8X4 = mybir.dt.float8_e4m3fn_x4
+FP4X4 = mybir.dt.float4_e2m1fn_x4
+ACT = mybir.ActivationFunctionType
+ALU = mybir.AluOpType
+
+P = 128
+TOKENS = 256
+FEATURES = 1024
+HEAD = 128
+PAIRS = HEAD // 2
+EPS = 1e-6
+
+K_PASS = 512
+PASSES = FEATURES // K_PASS
+TOKEN_TILES = TOKENS // P
+BANK = 512
+CHUNKS = FEATURES // BANK
+CHUNK_HEADS = BANK // HEAD
+GAIN_PAD = 256
+
+FLOPS = 2 * TOKENS * FEATURES * FEATURES
+
+
+def tile_selfattention_pa_s_kernel(tc, x, freqs, w_words, w_scales, b, g, out):
+    nc = tc.nc
+    x_rows = x.flatten_outer_dims()
+    freq_rows = freqs.rearrange("a s b j i c -> (a s b) (j i c)")
+    out_rows = out.rearrange("a s h d -> (a s) (h d)")
+
+    with ExitStack() as ctx:
+        keep = ctx.enter_context(tc.tile_pool(name="keep", bufs=1))
+        work = ctx.enter_context(tc.tile_pool(name="work", bufs=TOKEN_TILES * CHUNKS))
+        psum_keep = ctx.enter_context(tc.psum_pool(name="psum_keep", bufs=1))
+        psum_acc = ctx.enter_context(tc.psum_pool(name="psum_acc", bufs=3))
+
+        w_planes = keep.tile([P, PASSES, FEATURES], U8, align_bytes=64)
+        nc.vector.memset(w_planes[:].rearrange("p g n -> p (g n)").bitcast(I32), 0)
+        vec_row = keep.tile([P, FEATURES + GAIN_PAD], BF16)
+        nc.vector.memset(vec_row[:].bitcast(I32), 0)
+        ones = keep.tile([P, P], BF16)
+        nc.vector.memset(ones[:], 1.0)
+        one_col = keep.tile([P, 1], F32)
+        nc.vector.memset(one_col[:], 1.0)
+        ident = keep.tile([P, P], F32)
+        make_identity(nc, ident[:])
+
+        warm = keep.tile([P, 1], F32)
+        nc.scalar.activation(out=warm[:], in_=one_col[:], func=ACT.Abs_reciprocal_sqrt)
+
+        x_sb = [keep.tile([P, FEATURES], BF16, name="x_sb%d" % t) for t in range(TOKEN_TILES)]
+        w_sb = [
+            keep.tile([P, PASSES, 2 * BANK], U8, name="w_sb%d" % c, align_bytes=64)
+            for c in range(CHUNKS)
+        ]
+        freq_sb = keep.tile([P, TOKEN_TILES, 4 * PAIRS], BF16)
+        words_by_partition = w_words.bitcast(I32).rearrange("g p n -> p g n")
+        scales_by_row = w_scales.bitcast(I32).rearrange("g q n -> q g n")
+        chunk_i32 = 2 * BANK // 4
+
+        def load_w(c):
+            nc.sync.dma_start(
+                out=w_sb[c][:].bitcast(I32),
+                in_=words_by_partition[:, :, c * chunk_i32 : (c + 1) * chunk_i32],
+            )
+
+        nc.sync.dma_start(out=x_sb[0][:], in_=x_rows[0:P, :])
+        nc.sync.dma_start(out=vec_row[0:1, 0:FEATURES], in_=b.rearrange("(o n) -> o n", o=1))
+        nc.sync.dma_start(
+            out=vec_row[0:1, FEATURES : FEATURES + HEAD], in_=g.rearrange("(o n) -> o n", o=1)
+        )
+        for quad in range(4):
+            nc.sync.dma_start(
+                out=w_planes[32 * quad : 32 * quad + 4, :, :].bitcast(I32),
+                in_=scales_by_row[4 * quad : 4 * quad + 4, :, :],
+            )
+        load_w(0)
+        nc.sync.dma_start(
+            out=freq_sb[:], in_=freq_rows.rearrange("(t p) f -> p t f", p=P)
+        )
+        nc.sync.dma_start(out=x_sb[1][:], in_=x_rows[P : 2 * P, :])
+        load_w(1)
+
+        x_codes = [
+            keep.tile([P, PASSES * P], U32, name="x_codes%d" % t, align_bytes=64)
+            for t in range(TOKEN_TILES)
+        ]
+        x_planes = [
+            keep.tile([P, PASSES * P], U8, name="x_planes%d" % t, align_bytes=64)
+            for t in range(TOKEN_TILES)
+        ]
+
+        def quantise_tokens(t):
+            x_words = x_sb[t][:].bitcast(F32)
+            flipped = psum_keep.tile([P, PASSES, 2, P], F32, name="flipped%d" % t)
+            for gp in range(PASSES):
+                for u in range(2):
+                    first = gp * (K_PASS // 2) + u
+                    nc.tensor.transpose(
+                        flipped[:, gp, u, :],
+                        x_words[:, first : (gp + 1) * (K_PASS // 2) : 2],
+                        ident[:],
+                    )
+            grouped = keep.tile([P, PASSES * P * 4], BF16, name="grouped%d" % t, align_bytes=64)
+            nc.scalar.copy(
+                out=grouped[:].bitcast(F32).rearrange("p (g s u) -> p g s u", g=PASSES, u=2),
+                in_=flipped[:].rearrange("p g u s -> p g s u"),
+            )
+            nc.vector.quantize_mx(
+                out=x_codes[t][:].bitcast(FP8X4), scales=x_planes[t][:], in_=grouped[:]
+            )
+
+        bias_all = keep.tile([P, FEATURES], F32)
+
+        def spread_bias_and_gain():
+            for c in range(CHUNKS):
+                bias_ps = psum_keep.tile([P, BANK], F32, name="bias_ps%d" % c)
+                nc.tensor.matmul(
+                    bias_ps[:], lhsT=ones[:], rhs=vec_row[:, c * BANK : (c + 1) * BANK],
+                    start=True, stop=True,
+                )
+                nc.scalar.copy(out=bias_all[:, c * BANK : (c + 1) * BANK], in_=bias_ps[:])
+            gain_ps = psum_keep.tile([P, GAIN_PAD], F32)
+            nc.tensor.matmul(
+                gain_ps[:], lhsT=ones[:], rhs=vec_row[:, FEATURES : FEATURES + GAIN_PAD],
+                start=True, stop=True,
+            )
+            return gain_ps
+
+        table = [keep.tile([P, 2, HEAD], F32, name="table%d" % t) for t in range(TOKEN_TILES)]
+
+        def scale_table(t, gain_ps):
+            nc.vector.tensor_tensor(
+                out=table[t][:].rearrange("p c (j i) -> p c j i", i=2),
+                in0=freq_sb[:, t, :].rearrange("p (j i c) -> p c j i", i=2, c=2),
+                in1=gain_ps[:, 0:HEAD]
+                .rearrange("p (j c) -> p c j", c=2)
+                .unsqueeze(3)
+                .to_broadcast([P, 2, PAIRS, 2]),
+                op=ALU.mult,
+            )
+
+        def project(t, c):
+            acc = psum_acc.tile([P, BANK], F32)
+            for gp in range(PASSES):
+                nc.tensor.matmul_mx(
+                    out=acc[:],
+                    lhsT=x_codes[t][:, gp * P : (gp + 1) * P].bitcast(FP8X4),
+                    lhsT_scale=x_planes[t][:, gp * P : (gp + 1) * P],
+                    rhs=w_sb[c][:, gp, :].bitcast(FP4X4),
+                    rhs_scale=w_planes[:, gp, c * BANK : (c + 1) * BANK],
+                    start=(gp == 0),
+                    stop=(gp == PASSES - 1),
+                )
+            return acc
+
+        def finish(t, c, acc):
+            shape = [P, CHUNK_HEADS, PAIRS, 2]
+            u = work.tile([P, BANK], F32)
+            nc.vector.tensor_tensor(
+                out=u[:], in0=acc[:], in1=bias_all[:, c * BANK : (c + 1) * BANK], op=ALU.add
+            )
+            squares = work.tile([P, BANK], F32)
+            sums = work.tile([P, CHUNK_HEADS], F32)
+            for h in range(CHUNK_HEADS):
+                nc.scalar.activation(
+                    out=squares[:, h * HEAD : (h + 1) * HEAD],
+                    in_=u[:, h * HEAD : (h + 1) * HEAD],
+                    func=ACT.Square,
+                    accum_out=sums[:, h : h + 1],
+                )
+            rstd = work.tile([P, CHUNK_HEADS], F32)
+            nc.scalar.activation(
+                out=rstd[:], in_=sums[:], func=ACT.Abs_reciprocal_sqrt, scale=1.0 / HEAD, bias=EPS
+            )
+            u_pairs = u[:].rearrange("p (h j c) -> p h j c", h=CHUNK_HEADS, c=2)
+            parts = []
+            for cc in range(2):
+                part = work.tile([P, BANK], F32, name="part%d" % cc)
+                nc.vector.tensor_tensor(
+                    out=part[:].rearrange("p (h j i) -> p h j i", h=CHUNK_HEADS, i=2),
+                    in0=u_pairs[:, :, :, cc : cc + 1].to_broadcast(shape),
+                    in1=table[t][:, cc, :]
+                    .rearrange("p (j i) -> p j i", i=2)
+                    .unsqueeze(1)
+                    .to_broadcast(shape),
+                    op=ALU.mult,
+                )
+                parts.append(part)
+            rotated = work.tile([P, BANK], F32)
+            nc.vector.tensor_tensor(out=rotated[:], in0=parts[0][:], in1=parts[1][:], op=ALU.add)
+            result = work.tile([P, BANK], F32)
+            for h in range(CHUNK_HEADS):
+                nc.scalar.activation(
+                    out=result[:, h * HEAD : (h + 1) * HEAD],
+                    in_=rotated[:, h * HEAD : (h + 1) * HEAD],
+                    func=ACT.Copy,
+                    scale=rstd[:, h : h + 1],
+                )
+            nc.sync.dma_start(
+                out=out_rows[t * P : (t + 1) * P, c * BANK : (c + 1) * BANK], in_=result[:]
+            )
+
+        quantise_tokens(0)
+        gain_ps = spread_bias_and_gain()
+        scale_table(0, gain_ps)
+        quantise_tokens(1)
+        scale_table(1, gain_ps)
+        for t in range(TOKEN_TILES):
+            for c in range(CHUNKS):
+                finish(t, c, project(t, c))

@@ -26,6 +26,7 @@ TOKEN_TILES = TOKENS // P
 BANK = 512
 CHUNKS = FEATURES // BANK
 CHUNK_HEADS = BANK // HEAD
+HEADS = FEATURES // HEAD
 GAIN_PAD = 256
 
 FLOPS = 2 * TOKENS * FEATURES * FEATURES
@@ -39,57 +40,49 @@ def tile_selfattention_pa_s_kernel(tc, x, freqs, w_words, w_scales, b, g, out):
 
     with ExitStack() as ctx:
         keep = ctx.enter_context(tc.tile_pool(name="keep", bufs=1))
-        work = ctx.enter_context(tc.tile_pool(name="work", bufs=TOKEN_TILES * CHUNKS))
-        psum_keep = ctx.enter_context(tc.psum_pool(name="psum_keep", bufs=1))
-        psum_acc = ctx.enter_context(tc.psum_pool(name="psum_acc", bufs=3))
+        work = ctx.enter_context(tc.tile_pool(name="work", bufs=TOKEN_TILES))
+        psum_flip = ctx.enter_context(tc.psum_pool(name="psum_flip", bufs=TOKEN_TILES * PASSES))
+        psum_spread = ctx.enter_context(tc.psum_pool(name="psum_spread", bufs=2))
+        psum_acc = ctx.enter_context(tc.psum_pool(name="psum_acc", bufs=CHUNKS))
+        ctx.enter_context(tc.manual_schedule())
 
+        vec_row = keep.tile([P, FEATURES + GAIN_PAD], BF16)
+        nc.gpsimd.memset(vec_row[:].bitcast(F32), 0.0)
         w_planes = keep.tile([P, PASSES, FEATURES], U8, align_bytes=64)
         nc.vector.memset(w_planes[:].rearrange("p g n -> p (g n)").bitcast(I32), 0)
-        vec_row = keep.tile([P, FEATURES + GAIN_PAD], BF16)
-        nc.vector.memset(vec_row[:].bitcast(I32), 0)
-        ones = keep.tile([P, P], BF16)
-        nc.vector.memset(ones[:], 1.0)
-        one_col = keep.tile([P, 1], F32)
-        nc.vector.memset(one_col[:], 1.0)
-        ident = keep.tile([P, P], F32)
-        make_identity(nc, ident[:])
 
-        warm = keep.tile([P, 1], F32)
-        nc.scalar.activation(out=warm[:], in_=one_col[:], func=ACT.Abs_reciprocal_sqrt)
-
-        x_sb = [keep.tile([P, FEATURES], BF16, name="x_sb%d" % t) for t in range(TOKEN_TILES)]
-        w_sb = [
-            keep.tile([P, PASSES, 2 * BANK], U8, name="w_sb%d" % c, align_bytes=64)
-            for c in range(CHUNKS)
-        ]
+        x_sb = keep.tile([P, TOKEN_TILES, FEATURES], BF16)
         freq_sb = keep.tile([P, TOKEN_TILES, 4 * PAIRS], BF16)
-        words_by_partition = w_words.bitcast(I32).rearrange("g p n -> p g n")
-        scales_by_row = w_scales.bitcast(I32).rearrange("g q n -> q g n")
-        chunk_i32 = 2 * BANK // 4
-
-        def load_w(c):
-            nc.sync.dma_start(
-                out=w_sb[c][:].bitcast(I32),
-                in_=words_by_partition[:, :, c * chunk_i32 : (c + 1) * chunk_i32],
-            )
-
-        nc.sync.dma_start(out=x_sb[0][:], in_=x_rows[0:P, :])
-        nc.sync.dma_start(out=vec_row[0:1, 0:FEATURES], in_=b.rearrange("(o n) -> o n", o=1))
-        nc.sync.dma_start(
+        w_sb = keep.tile([P, PASSES, 2 * FEATURES], U8, align_bytes=64)
+        nc.scalar.dma_start(
             out=vec_row[0:1, FEATURES : FEATURES + HEAD], in_=g.rearrange("(o n) -> o n", o=1)
         )
+        nc.sync.dma_start(out=x_sb[:], in_=x_rows.rearrange("(t p) k -> p t k", p=P))
+        nc.sync.dma_start(out=freq_sb[:], in_=freq_rows.rearrange("(t p) f -> p t f", p=P))
+        scales_by_row = w_scales.bitcast(I32).rearrange("g q n -> q g n")
         for quad in range(4):
             nc.sync.dma_start(
                 out=w_planes[32 * quad : 32 * quad + 4, :, :].bitcast(I32),
                 in_=scales_by_row[4 * quad : 4 * quad + 4, :, :],
             )
-        load_w(0)
         nc.sync.dma_start(
-            out=freq_sb[:], in_=freq_rows.rearrange("(t p) f -> p t f", p=P)
+            out=w_sb[:].bitcast(I32), in_=w_words.bitcast(I32).rearrange("g p n -> p g n")
         )
-        nc.sync.dma_start(out=x_sb[1][:], in_=x_rows[P : 2 * P, :])
-        load_w(1)
+        nc.sync.dma_start(out=vec_row[0:1, 0:FEATURES], in_=b.rearrange("(o n) -> o n", o=1))
 
+        ident = keep.tile([P, P], F32)
+        make_identity(nc, ident[:])
+        ones = keep.tile([P, P], BF16)
+        nc.vector.memset(ones[:], 1.0)
+        one_col = keep.tile([P, 1], F32)
+        nc.vector.memset(one_col[:], 1.0)
+        warm = keep.tile([P, 1], F32)
+        nc.scalar.activation(out=warm[:], in_=one_col[:], func=ACT.Abs_reciprocal_sqrt)
+
+        grouped = [
+            keep.tile([P, PASSES, P, 4], BF16, name="grouped%d" % t, align_bytes=64)
+            for t in range(TOKEN_TILES)
+        ]
         x_codes = [
             keep.tile([P, PASSES * P], U32, name="x_codes%d" % t, align_bytes=64)
             for t in range(TOKEN_TILES)
@@ -99,50 +92,54 @@ def tile_selfattention_pa_s_kernel(tc, x, freqs, w_words, w_scales, b, g, out):
             for t in range(TOKEN_TILES)
         ]
 
-        def quantise_tokens(t):
-            x_words = x_sb[t][:].bitcast(F32)
-            flipped = psum_keep.tile([P, PASSES, 2, P], F32, name="flipped%d" % t)
+        def transpose_tokens(t):
+            x_words = x_sb[:, t, :].bitcast(F32)
+            banks = []
             for gp in range(PASSES):
+                flipped = psum_flip.tile([P, 2, P], F32, name="flipped")
                 for u in range(2):
                     first = gp * (K_PASS // 2) + u
                     nc.tensor.transpose(
-                        flipped[:, gp, u, :],
-                        x_words[:, first : (gp + 1) * (K_PASS // 2) : 2],
-                        ident[:],
+                        flipped[:, u, :], x_words[:, first : (gp + 1) * (K_PASS // 2) : 2], ident[:]
                     )
-            grouped = keep.tile([P, PASSES * P * 4], BF16, name="grouped%d" % t, align_bytes=64)
-            nc.scalar.copy(
-                out=grouped[:].bitcast(F32).rearrange("p (g s u) -> p g s u", g=PASSES, u=2),
-                in_=flipped[:].rearrange("p g u s -> p g s u"),
-            )
-            nc.vector.quantize_mx(
-                out=x_codes[t][:].bitcast(FP8X4), scales=x_planes[t][:], in_=grouped[:]
-            )
+                banks.append(flipped)
+            return banks
 
-        bias_all = keep.tile([P, FEATURES], F32)
-
-        def spread_bias_and_gain():
-            for c in range(CHUNKS):
-                bias_ps = psum_keep.tile([P, BANK], F32, name="bias_ps%d" % c)
-                nc.tensor.matmul(
-                    bias_ps[:], lhsT=ones[:], rhs=vec_row[:, c * BANK : (c + 1) * BANK],
-                    start=True, stop=True,
+        def regroup_tokens(t, banks):
+            for gp in range(PASSES):
+                nc.scalar.copy(
+                    out=grouped[t][:, gp, :, :].rearrange("p s v -> p (s v)").bitcast(F32)
+                    .rearrange("p (s u) -> p s u", u=2),
+                    in_=banks[gp][:].rearrange("p u s -> p s u"),
                 )
-                nc.scalar.copy(out=bias_all[:, c * BANK : (c + 1) * BANK], in_=bias_ps[:])
-            gain_ps = psum_keep.tile([P, GAIN_PAD], F32)
+
+        def quantise_tokens(t):
+            nc.vector.quantize_mx(
+                out=x_codes[t][:].bitcast(FP8X4),
+                scales=x_planes[t][:],
+                in_=grouped[t][:].rearrange("p g s v -> p (g s v)"),
+            )
+
+        def spread(first, width):
+            everywhere = psum_spread.tile([P, BANK], F32, name="everywhere")
             nc.tensor.matmul(
-                gain_ps[:], lhsT=ones[:], rhs=vec_row[:, FEATURES : FEATURES + GAIN_PAD],
+                everywhere[:, 0:width], lhsT=ones[:], rhs=vec_row[:, first : first + width],
                 start=True, stop=True,
             )
-            return gain_ps
+            return everywhere
+
+        bias_all = [keep.tile([P, BANK], F32, name="bias_all%d" % c) for c in range(CHUNKS)]
+
+        def spread_bias(c):
+            nc.scalar.copy(out=bias_all[c][:], in_=spread(c * BANK, BANK)[:])
 
         table = [keep.tile([P, 2, HEAD], F32, name="table%d" % t) for t in range(TOKEN_TILES)]
 
-        def scale_table(t, gain_ps):
+        def scale_table(t, gain):
             nc.vector.tensor_tensor(
                 out=table[t][:].rearrange("p c (j i) -> p c j i", i=2),
                 in0=freq_sb[:, t, :].rearrange("p (j i c) -> p c j i", i=2, c=2),
-                in1=gain_ps[:, 0:HEAD]
+                in1=gain[:, 0:HEAD]
                 .rearrange("p (j c) -> p c j", c=2)
                 .unsqueeze(3)
                 .to_broadcast([P, 2, PAIRS, 2]),
@@ -150,71 +147,89 @@ def tile_selfattention_pa_s_kernel(tc, x, freqs, w_words, w_scales, b, g, out):
             )
 
         def project(t, c):
-            acc = psum_acc.tile([P, BANK], F32)
+            acc = psum_acc.tile([P, BANK], F32, name="acc")
             for gp in range(PASSES):
                 nc.tensor.matmul_mx(
                     out=acc[:],
                     lhsT=x_codes[t][:, gp * P : (gp + 1) * P].bitcast(FP8X4),
                     lhsT_scale=x_planes[t][:, gp * P : (gp + 1) * P],
-                    rhs=w_sb[c][:, gp, :].bitcast(FP4X4),
+                    rhs=w_sb[:, gp, c * 2 * BANK : (c + 1) * 2 * BANK].bitcast(FP4X4),
                     rhs_scale=w_planes[:, gp, c * BANK : (c + 1) * BANK],
                     start=(gp == 0),
                     stop=(gp == PASSES - 1),
                 )
             return acc
 
-        def finish(t, c, acc):
+        def finish(t, sums_of, between):
             shape = [P, CHUNK_HEADS, PAIRS, 2]
-            u = work.tile([P, BANK], F32)
-            nc.vector.tensor_tensor(
-                out=u[:], in0=acc[:], in1=bias_all[:, c * BANK : (c + 1) * BANK], op=ALU.add
-            )
-            squares = work.tile([P, BANK], F32)
-            sums = work.tile([P, CHUNK_HEADS], F32)
-            for h in range(CHUNK_HEADS):
+            u = work.tile([P, CHUNKS, BANK], F32)
+            for c in range(CHUNKS):
+                nc.vector.tensor_tensor(
+                    out=u[:, c, :], in0=sums_of[c][:], in1=bias_all[c][:], op=ALU.add
+                )
+            between()
+            squares = work.tile([P, HEADS, HEAD], F32)
+            sums = work.tile([P, HEADS], F32)
+            u_heads = u[:].rearrange("p c (h d) -> p (c h) d", d=HEAD)
+            for h in range(HEADS):
                 nc.scalar.activation(
-                    out=squares[:, h * HEAD : (h + 1) * HEAD],
-                    in_=u[:, h * HEAD : (h + 1) * HEAD],
-                    func=ACT.Square,
+                    out=squares[:, h, :], in_=u_heads[:, h, :], func=ACT.Square,
                     accum_out=sums[:, h : h + 1],
                 )
-            rstd = work.tile([P, CHUNK_HEADS], F32)
+            rstd = work.tile([P, HEADS], F32)
             nc.scalar.activation(
                 out=rstd[:], in_=sums[:], func=ACT.Abs_reciprocal_sqrt, scale=1.0 / HEAD, bias=EPS
             )
-            u_pairs = u[:].rearrange("p (h j c) -> p h j c", h=CHUNK_HEADS, c=2)
-            parts = []
+            parts = [work.tile([P, CHUNKS, BANK], F32, name="part%d" % cc) for cc in range(2)]
             for cc in range(2):
-                part = work.tile([P, BANK], F32, name="part%d" % cc)
-                nc.vector.tensor_tensor(
-                    out=part[:].rearrange("p (h j i) -> p h j i", h=CHUNK_HEADS, i=2),
-                    in0=u_pairs[:, :, :, cc : cc + 1].to_broadcast(shape),
-                    in1=table[t][:, cc, :]
-                    .rearrange("p (j i) -> p j i", i=2)
-                    .unsqueeze(1)
-                    .to_broadcast(shape),
-                    op=ALU.mult,
-                )
-                parts.append(part)
-            rotated = work.tile([P, BANK], F32)
-            nc.vector.tensor_tensor(out=rotated[:], in0=parts[0][:], in1=parts[1][:], op=ALU.add)
-            result = work.tile([P, BANK], F32)
-            for h in range(CHUNK_HEADS):
-                nc.scalar.activation(
-                    out=result[:, h * HEAD : (h + 1) * HEAD],
-                    in_=rotated[:, h * HEAD : (h + 1) * HEAD],
-                    func=ACT.Copy,
-                    scale=rstd[:, h : h + 1],
-                )
-            nc.sync.dma_start(
-                out=out_rows[t * P : (t + 1) * P, c * BANK : (c + 1) * BANK], in_=result[:]
-            )
-
-        quantise_tokens(0)
-        gain_ps = spread_bias_and_gain()
-        scale_table(0, gain_ps)
-        quantise_tokens(1)
-        scale_table(1, gain_ps)
-        for t in range(TOKEN_TILES):
+                for c in range(CHUNKS):
+                    nc.vector.tensor_tensor(
+                        out=parts[cc][:, c, :].rearrange("p (h j i) -> p h j i", h=CHUNK_HEADS, i=2),
+                        in0=u[:, c, :]
+                        .rearrange("p (h j c) -> p h j c", h=CHUNK_HEADS, c=2)[:, :, :, cc : cc + 1]
+                        .to_broadcast(shape),
+                        in1=table[t][:, cc, :]
+                        .rearrange("p (j i) -> p j i", i=2)
+                        .unsqueeze(1)
+                        .to_broadcast(shape),
+                        op=ALU.mult,
+                    )
+            rotated = work.tile([P, CHUNKS, BANK], F32)
+            result = work.tile([P, CHUNKS, BANK], F32)
             for c in range(CHUNKS):
-                finish(t, c, project(t, c))
+                nc.vector.tensor_tensor(
+                    out=rotated[:, c, :], in0=parts[0][:, c, :], in1=parts[1][:, c, :], op=ALU.add
+                )
+            for c in range(CHUNKS):
+                for h in range(CHUNK_HEADS):
+                    nc.scalar.activation(
+                        out=result[:, c, h * HEAD : (h + 1) * HEAD],
+                        in_=rotated[:, c, h * HEAD : (h + 1) * HEAD],
+                        func=ACT.Copy,
+                        scale=rstd[:, c * CHUNK_HEADS + h : c * CHUNK_HEADS + h + 1],
+                    )
+                nc.sync.dma_start(
+                    out=out_rows[t * P : (t + 1) * P, c * BANK : (c + 1) * BANK],
+                    in_=result[:, c, :],
+                )
+
+        gain = spread(FEATURES, GAIN_PAD)
+        banks_of = [transpose_tokens(t) for t in range(TOKEN_TILES)]
+        for t in range(TOKEN_TILES):
+            regroup_tokens(t, banks_of[t])
+        for t in range(TOKEN_TILES):
+            scale_table(t, gain)
+        for t in range(TOKEN_TILES):
+            quantise_tokens(t)
+        first_sums = []
+        for c in range(CHUNKS):
+            spread_bias(c)
+            first_sums.append(project(0, c))
+        second_sums = []
+
+        def project_second():
+            for c in range(CHUNKS):
+                second_sums.append(project(1, c))
+
+        finish(0, first_sums, project_second)
+        finish(1, second_sums, lambda: None)

@@ -27,6 +27,8 @@ BANK = 512
 CHUNKS = FEATURES // BANK
 CHUNK_HEADS = BANK // HEAD
 HEADS = FEATURES // HEAD
+PIECE_HEADS = 2
+PIECE = PIECE_HEADS * HEAD
 GAIN_PAD = 256
 
 FLOPS = 2 * TOKENS * FEATURES * FEATURES
@@ -106,8 +108,9 @@ def tile_selfattention_pa_s_kernel(tc, x, freqs, w_words, w_scales, b, g, out):
             return banks
 
         def regroup_tokens(t, banks):
+            copy_of_pass = [nc.scalar.copy, nc.vector.tensor_copy]
             for gp in range(PASSES):
-                nc.scalar.copy(
+                copy_of_pass[gp](
                     out=grouped[t][:, gp, :, :].rearrange("p s v -> p (s v)").bitcast(F32)
                     .rearrange("p (s u) -> p s u", u=2),
                     in_=banks[gp][:].rearrange("p u s -> p s u"),
@@ -196,35 +199,38 @@ def tile_selfattention_pa_s_kernel(tc, x, freqs, w_words, w_scales, b, g, out):
                     )
             rotated = work.tile([P, CHUNKS, BANK], F32)
             result = work.tile([P, CHUNKS, BANK], F32)
-            for c in range(CHUNKS):
+            rotated_flat = rotated[:].rearrange("p c n -> p (c n)")
+            result_flat = result[:].rearrange("p c n -> p (c n)")
+            for first in range(0, FEATURES, PIECE):
                 nc.vector.tensor_tensor(
-                    out=rotated[:, c, :], in0=parts[0][:, c, :], in1=parts[1][:, c, :], op=ALU.add
+                    out=rotated_flat[:, first : first + PIECE],
+                    in0=parts[0][:].rearrange("p c n -> p (c n)")[:, first : first + PIECE],
+                    in1=parts[1][:].rearrange("p c n -> p (c n)")[:, first : first + PIECE],
+                    op=ALU.add,
                 )
-            for c in range(CHUNKS):
-                for h in range(CHUNK_HEADS):
+            for first in range(0, FEATURES, PIECE):
+                for h in range(first // HEAD, first // HEAD + PIECE_HEADS):
                     nc.scalar.activation(
-                        out=result[:, c, h * HEAD : (h + 1) * HEAD],
-                        in_=rotated[:, c, h * HEAD : (h + 1) * HEAD],
+                        out=result_flat[:, h * HEAD : (h + 1) * HEAD],
+                        in_=rotated_flat[:, h * HEAD : (h + 1) * HEAD],
                         func=ACT.Copy,
-                        scale=rstd[:, c * CHUNK_HEADS + h : c * CHUNK_HEADS + h + 1],
+                        scale=rstd[:, h : h + 1],
                     )
                 nc.sync.dma_start(
-                    out=out_rows[t * P : (t + 1) * P, c * BANK : (c + 1) * BANK],
-                    in_=result[:, c, :],
+                    out=out_rows[t * P : (t + 1) * P, first : first + PIECE],
+                    in_=result_flat[:, first : first + PIECE],
                 )
 
         gain = spread(FEATURES, GAIN_PAD)
         banks_of = [transpose_tokens(t) for t in range(TOKEN_TILES)]
         for t in range(TOKEN_TILES):
-            regroup_tokens(t, banks_of[t])
-        for t in range(TOKEN_TILES):
             scale_table(t, gain)
         for t in range(TOKEN_TILES):
+            regroup_tokens(t, banks_of[t])
             quantise_tokens(t)
-        first_sums = []
         for c in range(CHUNKS):
             spread_bias(c)
-            first_sums.append(project(0, c))
+        first_sums = [project(0, c) for c in range(CHUNKS)]
         second_sums = []
 
         def project_second():

@@ -163,63 +163,69 @@ def tile_selfattention_pa_s_kernel(tc, x, freqs, w_words, w_scales, b, g, out):
                 )
             return acc
 
-        def finish(t, sums_of, between):
-            shape = [P, CHUNK_HEADS, PAIRS, 2]
-            u = work.tile([P, CHUNKS, BANK], F32)
-            for c in range(CHUNKS):
-                nc.vector.tensor_tensor(
-                    out=u[:, c, :], in0=sums_of[c][:], in1=bias_all[c][:], op=ALU.add
-                )
-            between()
-            squares = work.tile([P, HEADS, HEAD], F32)
-            sums = work.tile([P, HEADS], F32)
-            u_heads = u[:].rearrange("p c (h d) -> p (c h) d", d=HEAD)
-            for h in range(HEADS):
+        shape = [P, CHUNK_HEADS, PAIRS, 2]
+        u = [work.tile([P, CHUNKS, BANK], F32, name="u") for t in range(TOKEN_TILES)]
+        squares = [work.tile([P, CHUNKS, BANK], F32, name="squares") for t in range(TOKEN_TILES)]
+        sums = [work.tile([P, HEADS], F32, name="sums") for t in range(TOKEN_TILES)]
+        rstd = [work.tile([P, HEADS], F32, name="rstd") for t in range(TOKEN_TILES)]
+        parts = [
+            [work.tile([P, FEATURES], F32, name="part%d" % cc) for cc in range(2)]
+            for t in range(TOKEN_TILES)
+        ]
+        rotated = [work.tile([P, FEATURES], F32, name="rotated") for t in range(TOKEN_TILES)]
+        result = [work.tile([P, FEATURES], F32, name="result") for t in range(TOKEN_TILES)]
+
+        def add_bias(t, c, acc):
+            nc.vector.tensor_tensor(out=u[t][:, c, :], in0=acc[:], in1=bias_all[c][:], op=ALU.add)
+
+        def square_sums(t, c):
+            for hh in range(CHUNK_HEADS):
+                h = c * CHUNK_HEADS + hh
                 nc.scalar.activation(
-                    out=squares[:, h, :], in_=u_heads[:, h, :], func=ACT.Square,
-                    accum_out=sums[:, h : h + 1],
+                    out=squares[t][:, c, hh * HEAD : (hh + 1) * HEAD],
+                    in_=u[t][:, c, hh * HEAD : (hh + 1) * HEAD],
+                    func=ACT.Square,
+                    accum_out=sums[t][:, h : h + 1],
                 )
-            rstd = work.tile([P, HEADS], F32)
+
+        def norm_factor(t):
             nc.scalar.activation(
-                out=rstd[:], in_=sums[:], func=ACT.Abs_reciprocal_sqrt, scale=1.0 / HEAD, bias=EPS
+                out=rstd[t][:], in_=sums[t][:], func=ACT.Abs_reciprocal_sqrt,
+                scale=1.0 / HEAD, bias=EPS,
             )
-            parts = [work.tile([P, CHUNKS, BANK], F32, name="part%d" % cc) for cc in range(2)]
+
+        def multiply(t, c):
             for cc in range(2):
-                for c in range(CHUNKS):
-                    nc.vector.tensor_tensor(
-                        out=parts[cc][:, c, :].rearrange("p (h j i) -> p h j i", h=CHUNK_HEADS, i=2),
-                        in0=u[:, c, :]
-                        .rearrange("p (h j c) -> p h j c", h=CHUNK_HEADS, c=2)[:, :, :, cc : cc + 1]
-                        .to_broadcast(shape),
-                        in1=table[t][:, cc, :]
-                        .rearrange("p (j i) -> p j i", i=2)
-                        .unsqueeze(1)
-                        .to_broadcast(shape),
-                        op=ALU.mult,
-                    )
-            rotated = work.tile([P, CHUNKS, BANK], F32)
-            result = work.tile([P, CHUNKS, BANK], F32)
-            rotated_flat = rotated[:].rearrange("p c n -> p (c n)")
-            result_flat = result[:].rearrange("p c n -> p (c n)")
-            for first in range(0, FEATURES, PIECE):
                 nc.vector.tensor_tensor(
-                    out=rotated_flat[:, first : first + PIECE],
-                    in0=parts[0][:].rearrange("p c n -> p (c n)")[:, first : first + PIECE],
-                    in1=parts[1][:].rearrange("p c n -> p (c n)")[:, first : first + PIECE],
-                    op=ALU.add,
+                    out=parts[t][cc][:, c * BANK : (c + 1) * BANK]
+                    .rearrange("p (h j i) -> p h j i", h=CHUNK_HEADS, i=2),
+                    in0=u[t][:, c, :]
+                    .rearrange("p (h j c) -> p h j c", h=CHUNK_HEADS, c=2)[:, :, :, cc : cc + 1]
+                    .to_broadcast(shape),
+                    in1=table[t][:, cc, :]
+                    .rearrange("p (j i) -> p j i", i=2)
+                    .unsqueeze(1)
+                    .to_broadcast(shape),
+                    op=ALU.mult,
                 )
-            for first in range(0, FEATURES, PIECE):
-                for h in range(first // HEAD, first // HEAD + PIECE_HEADS):
-                    nc.scalar.activation(
-                        out=result_flat[:, h * HEAD : (h + 1) * HEAD],
-                        in_=rotated_flat[:, h * HEAD : (h + 1) * HEAD],
-                        func=ACT.Copy,
-                        scale=rstd[:, h : h + 1],
-                    )
-                nc.sync.dma_start(
-                    out=out_rows[t * P : (t + 1) * P, first : first + PIECE],
-                    in_=result_flat[:, first : first + PIECE],
+
+        def add_products(engine, t, piece):
+            cols = slice(piece * PIECE, (piece + 1) * PIECE)
+            engine.tensor_tensor(
+                out=rotated[t][:, cols], in0=parts[t][0][:, cols], in1=parts[t][1][:, cols],
+                op=ALU.add,
+            )
+
+        def scale_and_store(t, piece):
+            for h in range(piece * PIECE_HEADS, (piece + 1) * PIECE_HEADS):
+                nc.scalar.activation(
+                    out=result[t][:, h * HEAD : (h + 1) * HEAD],
+                    in_=rotated[t][:, h * HEAD : (h + 1) * HEAD],
+                    func=ACT.Copy,
+                    scale=rstd[t][:, h : h + 1],
                 )
+            cols = slice(piece * PIECE, (piece + 1) * PIECE)
+            nc.sync.dma_start(out=out_rows[t * P : (t + 1) * P, cols], in_=result[t][:, cols])
 
         gain = spread(FEATURES, GAIN_PAD)
         banks_of = [transpose_tokens(t) for t in range(TOKEN_TILES)]
@@ -231,11 +237,28 @@ def tile_selfattention_pa_s_kernel(tc, x, freqs, w_words, w_scales, b, g, out):
         for c in range(CHUNKS):
             spread_bias(c)
         first_sums = [project(0, c) for c in range(CHUNKS)]
-        second_sums = []
-
-        def project_second():
-            for c in range(CHUNKS):
-                second_sums.append(project(1, c))
-
-        finish(0, first_sums, project_second)
-        finish(1, second_sums, lambda: None)
+        for c in range(CHUNKS):
+            add_bias(0, c, first_sums[c])
+        second_sums = [project(1, c) for c in range(CHUNKS)]
+        for c in range(CHUNKS):
+            square_sums(0, c)
+        norm_factor(0)
+        for c in range(CHUNKS):
+            multiply(0, c)
+            for piece in (2 * c, 2 * c + 1):
+                add_products(nc.gpsimd, 0, piece)
+        for c in range(CHUNKS):
+            add_bias(1, c, second_sums[c])
+        for c in range(CHUNKS):
+            scale_and_store(0, 2 * c)
+            scale_and_store(0, 2 * c + 1)
+            square_sums(1, c)
+        norm_factor(1)
+        multiply(1, 0)
+        add_products(nc.gpsimd, 1, 0)
+        add_products(nc.gpsimd, 1, 1)
+        multiply(1, 1)
+        add_products(nc.vector, 1, 2)
+        add_products(nc.vector, 1, 3)
+        for piece in range(FEATURES // PIECE):
+            scale_and_store(1, piece)

@@ -43,8 +43,8 @@ def tile_selfattention_pa_s_kernel(tc, x, freqs, w_words, w_scales, b, g, out):
     with ExitStack() as ctx:
         keep = ctx.enter_context(tc.tile_pool(name="keep", bufs=1))
         work = ctx.enter_context(tc.tile_pool(name="work", bufs=TOKEN_TILES))
-        psum_flip = ctx.enter_context(tc.psum_pool(name="psum_flip", bufs=TOKEN_TILES * PASSES))
-        psum_spread = ctx.enter_context(tc.psum_pool(name="psum_spread", bufs=2))
+        psum_short = ctx.enter_context(tc.psum_pool(name="psum_short", bufs=5))
+        psum_table = ctx.enter_context(tc.psum_pool(name="psum_table", bufs=1))
         psum_acc = ctx.enter_context(tc.psum_pool(name="psum_acc", bufs=CHUNKS))
         ctx.enter_context(tc.manual_schedule())
 
@@ -98,7 +98,7 @@ def tile_selfattention_pa_s_kernel(tc, x, freqs, w_words, w_scales, b, g, out):
             x_words = x_sb[:, t, :].bitcast(F32)
             banks = []
             for gp in range(PASSES):
-                flipped = psum_flip.tile([P, 2, P], F32, name="flipped")
+                flipped = psum_short.tile([P, 2, P], F32, name="short")
                 for u in range(2):
                     first = gp * (K_PASS // 2) + u
                     nc.tensor.transpose(
@@ -124,7 +124,7 @@ def tile_selfattention_pa_s_kernel(tc, x, freqs, w_words, w_scales, b, g, out):
             )
 
         def spread(first, width):
-            everywhere = psum_spread.tile([P, BANK], F32, name="everywhere")
+            everywhere = psum_short.tile([P, BANK], F32, name="short")
             nc.tensor.matmul(
                 everywhere[:, 0:width], lhsT=ones[:], rhs=vec_row[:, first : first + width],
                 start=True, stop=True,
@@ -148,6 +148,23 @@ def tile_selfattention_pa_s_kernel(tc, x, freqs, w_words, w_scales, b, g, out):
                 .to_broadcast([P, 2, PAIRS, 2]),
                 op=ALU.mult,
             )
+
+        table_flipped = keep.tile([P, TOKEN_TILES, 2, P], F32)
+        table_psum = psum_table.tile([P, TOKEN_TILES, 2, HEAD], F32)
+
+        def flip_tables():
+            flipped = psum_short.tile([P, TOKEN_TILES, 2, P], F32, name="short")
+            for t in range(TOKEN_TILES):
+                for cc in range(2):
+                    nc.tensor.transpose(flipped[:, t, cc, :], table[t][:, cc, :], ident[:])
+            return flipped
+
+        def keep_flipped_table(t, flipped):
+            nc.scalar.copy(out=table_flipped[:, t, :, :], in_=flipped[:, t, :, :])
+
+        def flip_table_back(t):
+            for cc in range(2):
+                nc.tensor.transpose(table_psum[:, t, cc, :], table_flipped[:, t, cc, :], ident[:])
 
         def project(t, c):
             acc = psum_acc.tile([P, BANK], F32, name="acc")
@@ -202,7 +219,7 @@ def tile_selfattention_pa_s_kernel(tc, x, freqs, w_words, w_scales, b, g, out):
                     in0=u[t][:, c, :]
                     .rearrange("p (h j c) -> p h j c", h=CHUNK_HEADS, c=2)[:, :, :, cc : cc + 1]
                     .to_broadcast(shape),
-                    in1=table[t][:, cc, :]
+                    in1=table_psum[:, t, cc, :]
                     .rearrange("p (j i) -> p j i", i=2)
                     .unsqueeze(1)
                     .to_broadcast(shape),
@@ -236,7 +253,12 @@ def tile_selfattention_pa_s_kernel(tc, x, freqs, w_words, w_scales, b, g, out):
             quantise_tokens(t)
         for c in range(CHUNKS):
             spread_bias(c)
+        tables_flipped = flip_tables()
+        for t in range(TOKEN_TILES):
+            keep_flipped_table(t, tables_flipped)
         first_sums = [project(0, c) for c in range(CHUNKS)]
+        for t in range(TOKEN_TILES):
+            flip_table_back(t)
         for c in range(CHUNKS):
             add_bias(0, c, first_sums[c])
         second_sums = [project(1, c) for c in range(CHUNKS)]

@@ -49,7 +49,10 @@ def tile_selfattention_pa_s_kernel(tc, x, freqs, w_words, w_scales, b, g, out):
         ctx.enter_context(tc.manual_schedule())
 
         vec_row = keep.tile([P, FEATURES + GAIN_PAD], BF16)
-        nc.gpsimd.memset(vec_row[:].bitcast(F32), 0.0)
+        nc.vector.memset(vec_row[:].bitcast(F32), 0.0)
+        ident = keep.tile([P, P], F32)
+        make_identity(nc, ident[:])
+        nc.gpsimd.dma_start(out=vec_row[0:1, 0:FEATURES], in_=b.rearrange("(o n) -> o n", o=1))
         w_planes = keep.tile([P, PASSES, FEATURES], U8, align_bytes=64)
         nc.vector.memset(w_planes[:].rearrange("p g n -> p (g n)").bitcast(I32), 0)
 
@@ -70,10 +73,7 @@ def tile_selfattention_pa_s_kernel(tc, x, freqs, w_words, w_scales, b, g, out):
         nc.sync.dma_start(
             out=w_sb[:].bitcast(I32), in_=w_words.bitcast(I32).rearrange("g p n -> p g n")
         )
-        nc.sync.dma_start(out=vec_row[0:1, 0:FEATURES], in_=b.rearrange("(o n) -> o n", o=1))
 
-        ident = keep.tile([P, P], F32)
-        make_identity(nc, ident[:])
         ones = keep.tile([P, P], BF16)
         nc.vector.memset(ones[:], 1.0)
         one_col = keep.tile([P, 1], F32)
@@ -211,23 +211,20 @@ def tile_selfattention_pa_s_kernel(tc, x, freqs, w_words, w_scales, b, g, out):
                 scale=1.0 / HEAD, bias=EPS,
             )
 
-        def multiply(t, c):
-            for cc in range(2):
-                nc.vector.tensor_tensor(
-                    out=parts[t][cc][:, c * BANK : (c + 1) * BANK]
-                    .rearrange("p (h j i) -> p h j i", h=CHUNK_HEADS, i=2),
-                    in0=u[t][:, c, :]
-                    .rearrange("p (h j c) -> p h j c", h=CHUNK_HEADS, c=2)[:, :, :, cc : cc + 1]
-                    .to_broadcast(shape),
-                    in1=table_psum[:, t, cc, :]
-                    .rearrange("p (j i) -> p j i", i=2)
-                    .unsqueeze(1)
-                    .to_broadcast(shape),
-                    op=ALU.mult,
-                )
+        def multiply(engine, t, c, cc, in_psum=True):
+            factors = table_psum[:, t, cc, :] if in_psum else table[t][:, cc, :]
+            engine.tensor_tensor(
+                out=parts[t][cc][:, c * BANK : (c + 1) * BANK]
+                .rearrange("p (h j i) -> p h j i", h=CHUNK_HEADS, i=2),
+                in0=u[t][:, c, :]
+                .rearrange("p (h j c) -> p h j c", h=CHUNK_HEADS, c=2)[:, :, :, cc : cc + 1]
+                .to_broadcast(shape),
+                in1=factors.rearrange("p (j i) -> p j i", i=2).unsqueeze(1).to_broadcast(shape),
+                op=ALU.mult,
+            )
 
-        def add_products(engine, t, piece):
-            cols = slice(piece * PIECE, (piece + 1) * PIECE)
+        def add_products(engine, t, piece, pieces=1):
+            cols = slice(piece * PIECE, (piece + pieces) * PIECE)
             engine.tensor_tensor(
                 out=rotated[t][:, cols], in0=parts[t][0][:, cols], in1=parts[t][1][:, cols],
                 op=ALU.add,
@@ -265,10 +262,12 @@ def tile_selfattention_pa_s_kernel(tc, x, freqs, w_words, w_scales, b, g, out):
         for c in range(CHUNKS):
             square_sums(0, c)
         norm_factor(0)
-        for c in range(CHUNKS):
-            multiply(0, c)
-            for piece in (2 * c, 2 * c + 1):
-                add_products(nc.gpsimd, 0, piece)
+        multiply(nc.gpsimd, 0, 0, 1, in_psum=False)
+        multiply(nc.vector, 0, 0, 0)
+        add_products(nc.gpsimd, 0, 0, 2)
+        multiply(nc.vector, 0, 1, 0)
+        multiply(nc.vector, 0, 1, 1)
+        add_products(nc.gpsimd, 0, 2, 2)
         for c in range(CHUNKS):
             add_bias(1, c, second_sums[c])
         for c in range(CHUNKS):
@@ -276,10 +275,12 @@ def tile_selfattention_pa_s_kernel(tc, x, freqs, w_words, w_scales, b, g, out):
             scale_and_store(0, 2 * c + 1)
             square_sums(1, c)
         norm_factor(1)
-        multiply(1, 0)
+        multiply(nc.vector, 1, 0, 0)
+        multiply(nc.vector, 1, 0, 1)
         add_products(nc.gpsimd, 1, 0)
         add_products(nc.gpsimd, 1, 1)
-        multiply(1, 1)
+        multiply(nc.vector, 1, 1, 0)
+        multiply(nc.vector, 1, 1, 1)
         add_products(nc.vector, 1, 2)
         add_products(nc.vector, 1, 3)
         for piece in range(FEATURES // PIECE):

@@ -29,7 +29,9 @@ CHUNK_HEADS = BANK // HEAD
 HEADS = FEATURES // HEAD
 PIECE_HEADS = 2
 PIECE = PIECE_HEADS * HEAD
-GAIN_PAD = 256
+
+WARM_MATMULS = 3
+WARM_TRANSPOSES = 4
 
 FLOPS = 2 * TOKENS * FEATURES * FEATURES
 
@@ -48,21 +50,21 @@ def tile_selfattention_pa_s_kernel(tc, x, freqs, w_words, w_scales, b, g, out):
         psum_acc = ctx.enter_context(tc.psum_pool(name="psum_acc", bufs=CHUNKS))
         ctx.enter_context(tc.manual_schedule())
 
-        vec_row = keep.tile([P, FEATURES + GAIN_PAD], BF16)
-        nc.vector.memset(vec_row[:].bitcast(F32), 0.0)
+        g_row = keep.tile([P, HEAD], BF16)
+        nc.gpsimd.memset(g_row[:].bitcast(F32), 0.0)
+        b_row = keep.tile([P, FEATURES], BF16)
+        nc.vector.memset(b_row[:].bitcast(F32), 0.0)
         ident = keep.tile([P, P], F32)
         make_identity(nc, ident[:])
-        nc.gpsimd.dma_start(out=vec_row[0:1, 0:FEATURES], in_=b.rearrange("(o n) -> o n", o=1))
+        nc.gpsimd.dma_start(out=b_row[0:1, :], in_=b.rearrange("(o n) -> o n", o=1))
         w_planes = keep.tile([P, PASSES, FEATURES], U8, align_bytes=64)
         nc.vector.memset(w_planes[:].rearrange("p g n -> p (g n)").bitcast(I32), 0)
 
         x_sb = keep.tile([P, TOKEN_TILES, FEATURES], BF16)
         freq_sb = keep.tile([P, TOKEN_TILES, 4 * PAIRS], BF16)
         w_sb = keep.tile([P, PASSES, 2 * FEATURES], U8, align_bytes=64)
-        nc.scalar.dma_start(
-            out=vec_row[0:1, FEATURES : FEATURES + HEAD], in_=g.rearrange("(o n) -> o n", o=1)
-        )
         nc.sync.dma_start(out=x_sb[:], in_=x_rows.rearrange("(t p) k -> p t k", p=P))
+        nc.sync.dma_start(out=g_row[0:1, :], in_=g.rearrange("(o n) -> o n", o=1))
         nc.sync.dma_start(out=freq_sb[:], in_=freq_rows.rearrange("(t p) f -> p t f", p=P))
         scales_by_row = w_scales.bitcast(I32).rearrange("g q n -> q g n")
         for quad in range(4):
@@ -74,6 +76,11 @@ def tile_selfattention_pa_s_kernel(tc, x, freqs, w_words, w_scales, b, g, out):
             out=w_sb[:].bitcast(I32), in_=w_words.bitcast(I32).rearrange("g p n -> p g n")
         )
 
+        idle_bank = psum_table.tile([P, TOKEN_TILES, 2, HEAD], F32, name="table_psum")
+        for i in range(WARM_MATMULS):
+            nc.tensor.matmul(idle_bank[:, 0, 0, :], lhsT=ident[:], rhs=ident[:], start=True, stop=True)
+        for i in range(WARM_TRANSPOSES):
+            nc.tensor.transpose(idle_bank[:, 0, 0, :], ident[:], ident[:])
         ones = keep.tile([P, P], BF16)
         nc.vector.memset(ones[:], 1.0)
         one_col = keep.tile([P, 1], F32)
@@ -123,18 +130,18 @@ def tile_selfattention_pa_s_kernel(tc, x, freqs, w_words, w_scales, b, g, out):
                 in_=grouped[t][:].rearrange("p g s v -> p (g s v)"),
             )
 
-        def spread(first, width):
-            everywhere = psum_short.tile([P, BANK], F32, name="short")
-            nc.tensor.matmul(
-                everywhere[:, 0:width], lhsT=ones[:], rhs=vec_row[:, first : first + width],
-                start=True, stop=True,
-            )
+        def spread_gain():
+            everywhere = psum_short.tile([P, HEAD], F32, name="short")
+            nc.tensor.matmul(everywhere[:], lhsT=ones[:], rhs=g_row[:], start=True, stop=True)
             return everywhere
 
-        bias_all = [keep.tile([P, BANK], F32, name="bias_all%d" % c) for c in range(CHUNKS)]
+        bias_all = keep.tile([P, FEATURES], BF16)
 
         def spread_bias(c):
-            nc.scalar.copy(out=bias_all[c][:], in_=spread(c * BANK, BANK)[:])
+            cols = slice(c * BANK, (c + 1) * BANK)
+            everywhere = psum_short.tile([P, BANK], BF16, name="short")
+            nc.tensor.matmul(everywhere[:], lhsT=ones[:], rhs=b_row[:, cols], start=True, stop=True)
+            nc.scalar.copy(out=bias_all[:, cols], in_=everywhere[:])
 
         table = [keep.tile([P, 2, HEAD], F32, name="table%d" % t) for t in range(TOKEN_TILES)]
 
@@ -150,7 +157,7 @@ def tile_selfattention_pa_s_kernel(tc, x, freqs, w_words, w_scales, b, g, out):
             )
 
         table_flipped = keep.tile([P, TOKEN_TILES, 2, P], F32)
-        table_psum = psum_table.tile([P, TOKEN_TILES, 2, HEAD], F32)
+        table_psum = psum_table.tile([P, TOKEN_TILES, 2, HEAD], F32, name="table_psum")
 
         def flip_tables():
             flipped = psum_short.tile([P, TOKEN_TILES, 2, P], F32, name="short")
@@ -193,7 +200,10 @@ def tile_selfattention_pa_s_kernel(tc, x, freqs, w_words, w_scales, b, g, out):
         result = [work.tile([P, FEATURES], F32, name="result") for t in range(TOKEN_TILES)]
 
         def add_bias(t, c, acc):
-            nc.vector.tensor_tensor(out=u[t][:, c, :], in0=acc[:], in1=bias_all[c][:], op=ALU.add)
+            nc.vector.tensor_tensor(
+                out=u[t][:, c, :], in0=acc[:], in1=bias_all[:, c * BANK : (c + 1) * BANK],
+                op=ALU.add,
+            )
 
         def square_sums(t, c):
             for hh in range(CHUNK_HEADS):
@@ -241,7 +251,7 @@ def tile_selfattention_pa_s_kernel(tc, x, freqs, w_words, w_scales, b, g, out):
             cols = slice(piece * PIECE, (piece + 1) * PIECE)
             nc.sync.dma_start(out=out_rows[t * P : (t + 1) * P, cols], in_=result[t][:, cols])
 
-        gain = spread(FEATURES, GAIN_PAD)
+        gain = spread_gain()
         banks_of = [transpose_tokens(t) for t in range(TOKEN_TILES)]
         for t in range(TOKEN_TILES):
             scale_table(t, gain)

@@ -187,6 +187,50 @@ def tile_selfattention_pa_s_kernel(tc, x, freqs, w_words, w_scales, b, g, out):
                 )
             return acc
 
+        bias_columns = keep.tile([P, CHUNK_HEADS], F32)
+        values_flipped = keep.tile([P, CHUNK_HEADS, P], F32)
+
+        def bias_to_partitions(c):
+            columns = psum_short.tile([P, CHUNK_HEADS], F32, name="short")
+            for hh in range(CHUNK_HEADS):
+                h = c * CHUNK_HEADS + hh
+                nc.tensor.matmul(
+                    columns[:, hh : hh + 1], lhsT=b_row[:, h * HEAD : (h + 1) * HEAD],
+                    rhs=ones[:, 0:1], start=True, stop=True,
+                )
+            return columns
+
+        def project_flipped(t, c):
+            flipped = psum_short.tile([P, CHUNK_HEADS, P], F32, name="short")
+            for hh in range(CHUNK_HEADS):
+                h = c * CHUNK_HEADS + hh
+                for gp in range(PASSES):
+                    nc.tensor.matmul_mx(
+                        out=flipped[:, hh, :],
+                        lhsT=w_sb[:, gp, 2 * h * HEAD : 2 * (h + 1) * HEAD].bitcast(FP4X4),
+                        lhsT_scale=w_planes[:, gp, h * HEAD : (h + 1) * HEAD],
+                        rhs=x_codes[t][:, gp * P : (gp + 1) * P].bitcast(FP8X4),
+                        rhs_scale=x_planes[t][:, gp * P : (gp + 1) * P],
+                        start=(gp == 0),
+                        stop=(gp == PASSES - 1),
+                    )
+            return flipped
+
+        def add_bias_flipped(flipped):
+            for hh in range(CHUNK_HEADS):
+                nc.scalar.activation(
+                    out=values_flipped[:, hh, :], in_=flipped[:, hh, :], func=ACT.Identity,
+                    bias=bias_columns[:, hh : hh + 1],
+                )
+
+        def flip_values_back():
+            values = psum_acc.tile([P, BANK], F32, name="acc")
+            for hh in range(CHUNK_HEADS):
+                nc.tensor.transpose(
+                    values[:, hh * HEAD : (hh + 1) * HEAD], values_flipped[:, hh, :], ident[:]
+                )
+            return values
+
         shape = [P, CHUNK_HEADS, PAIRS, 2]
         u = [work.tile([P, CHUNKS, BANK], F32, name="u") for t in range(TOKEN_TILES)]
         squares = [work.tile([P, CHUNKS, BANK], F32, name="squares") for t in range(TOKEN_TILES)]
@@ -205,12 +249,13 @@ def tile_selfattention_pa_s_kernel(tc, x, freqs, w_words, w_scales, b, g, out):
                 op=ALU.add,
             )
 
-        def square_sums(t, c):
+        def square_sums(t, c, values=None):
+            chunk = u[t][:, c, :] if values is None else values[:]
             for hh in range(CHUNK_HEADS):
                 h = c * CHUNK_HEADS + hh
                 nc.scalar.activation(
                     out=squares[t][:, c, hh * HEAD : (hh + 1) * HEAD],
-                    in_=u[t][:, c, hh * HEAD : (hh + 1) * HEAD],
+                    in_=chunk[:, hh * HEAD : (hh + 1) * HEAD],
                     func=ACT.Square,
                     accum_out=sums[t][:, h : h + 1],
                 )
@@ -221,12 +266,12 @@ def tile_selfattention_pa_s_kernel(tc, x, freqs, w_words, w_scales, b, g, out):
                 scale=1.0 / HEAD, bias=EPS,
             )
 
-        def multiply(engine, t, c, cc, in_psum=True):
+        def multiply(engine, t, c, cc, in_psum=True, values=None):
             factors = table_psum[:, t, cc, :] if in_psum else table[t][:, cc, :]
             engine.tensor_tensor(
                 out=parts[t][cc][:, c * BANK : (c + 1) * BANK]
                 .rearrange("p (h j i) -> p h j i", h=CHUNK_HEADS, i=2),
-                in0=u[t][:, c, :]
+                in0=(u[t][:, c, :] if values is None else values[:])
                 .rearrange("p (h j c) -> p h j c", h=CHUNK_HEADS, c=2)[:, :, :, cc : cc + 1]
                 .to_broadcast(shape),
                 in1=factors.rearrange("p (j i) -> p j i", i=2).unsqueeze(1).to_broadcast(shape),
@@ -268,29 +313,36 @@ def tile_selfattention_pa_s_kernel(tc, x, freqs, w_words, w_scales, b, g, out):
             flip_table_back(t)
         for c in range(CHUNKS):
             add_bias(0, c, first_sums[c])
-        second_sums = [project(1, c) for c in range(CHUNKS)]
+        last = CHUNKS - 1
+        second_sums = project(1, 0)
+        bias_in_psum = bias_to_partitions(last)
+        last_flipped = project_flipped(1, last)
         for c in range(CHUNKS):
             square_sums(0, c)
         norm_factor(0)
+        nc.scalar.copy(out=bias_columns[:], in_=bias_in_psum[:])
+        add_bias_flipped(last_flipped)
+        last_values = flip_values_back()
         multiply(nc.gpsimd, 0, 0, 1, in_psum=False)
         multiply(nc.vector, 0, 0, 0)
         add_products(nc.gpsimd, 0, 0, 2)
         multiply(nc.vector, 0, 1, 0)
         multiply(nc.vector, 0, 1, 1)
         add_products(nc.gpsimd, 0, 2, 2)
-        for c in range(CHUNKS):
-            add_bias(1, c, second_sums[c])
-        for c in range(CHUNKS):
-            scale_and_store(0, 2 * c)
-            scale_and_store(0, 2 * c + 1)
-            square_sums(1, c)
+        add_bias(1, 0, second_sums)
+        scale_and_store(0, 0)
+        scale_and_store(0, 1)
+        square_sums(1, last, values=last_values)
+        square_sums(1, 0)
         norm_factor(1)
+        scale_and_store(0, 2)
+        scale_and_store(0, 3)
         multiply(nc.vector, 1, 0, 0)
         multiply(nc.vector, 1, 0, 1)
         add_products(nc.gpsimd, 1, 0)
         add_products(nc.gpsimd, 1, 1)
-        multiply(nc.vector, 1, 1, 0)
-        multiply(nc.vector, 1, 1, 1)
+        multiply(nc.vector, 1, last, 0, in_psum=False, values=last_values)
+        multiply(nc.vector, 1, last, 1, in_psum=False, values=last_values)
         add_products(nc.vector, 1, 2)
         add_products(nc.vector, 1, 3)
         for piece in range(FEATURES // PIECE):

@@ -45,8 +45,8 @@ def tile_selfattention_pa_s_kernel(tc, x, freqs, w_words, w_scales, b, g, out):
     with ExitStack() as ctx:
         keep = ctx.enter_context(tc.tile_pool(name="keep", bufs=1))
         work = ctx.enter_context(tc.tile_pool(name="work", bufs=TOKEN_TILES))
-        psum_short = ctx.enter_context(tc.psum_pool(name="psum_short", bufs=5))
-        psum_table = ctx.enter_context(tc.psum_pool(name="psum_table", bufs=1))
+        psum_short = ctx.enter_context(tc.psum_pool(name="psum_short", bufs=4))
+        psum_table = ctx.enter_context(tc.psum_pool(name="psum_table", bufs=TOKEN_TILES))
         psum_acc = ctx.enter_context(tc.psum_pool(name="psum_acc", bufs=CHUNKS))
         ctx.enter_context(tc.manual_schedule())
 
@@ -76,11 +76,11 @@ def tile_selfattention_pa_s_kernel(tc, x, freqs, w_words, w_scales, b, g, out):
             out=w_sb[:].bitcast(I32), in_=w_words.bitcast(I32).rearrange("g p n -> p g n")
         )
 
-        idle_bank = psum_table.tile([P, TOKEN_TILES, 2, HEAD], F32, name="table_psum")
+        idle_bank = psum_acc.tile([P, BANK], F32, name="acc")
         for i in range(WARM_MATMULS):
-            nc.tensor.matmul(idle_bank[:, 0, 0, :], lhsT=ident[:], rhs=ident[:], start=True, stop=True)
+            nc.tensor.matmul(idle_bank[:, 0:P], lhsT=ident[:], rhs=ident[:], start=True, stop=True)
         for i in range(WARM_TRANSPOSES):
-            nc.tensor.transpose(idle_bank[:, 0, 0, :], ident[:], ident[:])
+            nc.tensor.transpose(idle_bank[:, 0:P], ident[:], ident[:])
         ones = keep.tile([P, P], BF16)
         nc.vector.memset(ones[:], 1.0)
         one_col = keep.tile([P, 1], F32)
@@ -115,7 +115,7 @@ def tile_selfattention_pa_s_kernel(tc, x, freqs, w_words, w_scales, b, g, out):
             return banks
 
         def regroup_tokens(t, banks):
-            copy_of_pass = [nc.scalar.copy, nc.vector.tensor_copy]
+            copy_of_pass = [nc.scalar.copy, nc.vector.tensor_copy if t == 0 else nc.scalar.copy]
             for gp in range(PASSES):
                 copy_of_pass[gp](
                     out=grouped[t][:, gp, :, :].rearrange("p s v -> p (s v)").bitcast(F32)
@@ -157,21 +157,20 @@ def tile_selfattention_pa_s_kernel(tc, x, freqs, w_words, w_scales, b, g, out):
             )
 
         table_flipped = keep.tile([P, TOKEN_TILES, 2, P], F32)
-        table_psum = psum_table.tile([P, TOKEN_TILES, 2, HEAD], F32, name="table_psum")
+        table_psum = [
+            psum_table.tile([P, 2, HEAD], F32, name="table_psum") for t in range(TOKEN_TILES)
+        ]
 
-        def flip_tables():
-            flipped = psum_short.tile([P, TOKEN_TILES, 2, P], F32, name="short")
-            for t in range(TOKEN_TILES):
-                for cc in range(2):
-                    nc.tensor.transpose(flipped[:, t, cc, :], table[t][:, cc, :], ident[:])
-            return flipped
+        def flip_table(t, flipped):
+            for cc in range(2):
+                nc.tensor.transpose(flipped[:, t, cc, :], table[t][:, cc, :], ident[:])
 
         def keep_flipped_table(t, flipped):
             nc.scalar.copy(out=table_flipped[:, t, :, :], in_=flipped[:, t, :, :])
 
         def flip_table_back(t):
             for cc in range(2):
-                nc.tensor.transpose(table_psum[:, t, cc, :], table_flipped[:, t, cc, :], ident[:])
+                nc.tensor.transpose(table_psum[t][:, cc, :], table_flipped[:, t, cc, :], ident[:])
 
         def project(t, c):
             acc = psum_acc.tile([P, BANK], F32, name="acc")
@@ -267,7 +266,7 @@ def tile_selfattention_pa_s_kernel(tc, x, freqs, w_words, w_scales, b, g, out):
             )
 
         def multiply(engine, t, c, cc, in_psum=True, values=None):
-            factors = table_psum[:, t, cc, :] if in_psum else table[t][:, cc, :]
+            factors = table_psum[t][:, cc, :] if in_psum else table[t][:, cc, :]
             engine.tensor_tensor(
                 out=parts[t][cc][:, c * BANK : (c + 1) * BANK]
                 .rearrange("p (h j i) -> p h j i", h=CHUNK_HEADS, i=2),
@@ -297,28 +296,32 @@ def tile_selfattention_pa_s_kernel(tc, x, freqs, w_words, w_scales, b, g, out):
             nc.sync.dma_start(out=out_rows[t * P : (t + 1) * P, cols], in_=result[t][:, cols])
 
         gain = spread_gain()
-        banks_of = [transpose_tokens(t) for t in range(TOKEN_TILES)]
+        banks_of = [transpose_tokens(0)]
         for t in range(TOKEN_TILES):
             scale_table(t, gain)
+        banks_of.append(transpose_tokens(1))
         for t in range(TOKEN_TILES):
             regroup_tokens(t, banks_of[t])
             quantise_tokens(t)
-        for c in range(CHUNKS):
-            spread_bias(c)
-        tables_flipped = flip_tables()
-        for t in range(TOKEN_TILES):
-            keep_flipped_table(t, tables_flipped)
-        first_sums = [project(0, c) for c in range(CHUNKS)]
-        for t in range(TOKEN_TILES):
-            flip_table_back(t)
+        spread_bias(0)
+        tables_flipped = psum_short.tile([P, TOKEN_TILES, 2, P], F32, name="short")
+        flip_table(0, tables_flipped)
+        keep_flipped_table(0, tables_flipped)
+        first_sums = [project(0, 0)]
+        spread_bias(1)
+        first_sums.append(project(0, 1))
+        flip_table_back(0)
+        flip_table(1, tables_flipped)
         for c in range(CHUNKS):
             add_bias(0, c, first_sums[c])
         last = CHUNKS - 1
         second_sums = project(1, 0)
         bias_in_psum = bias_to_partitions(last)
         last_flipped = project_flipped(1, last)
-        for c in range(CHUNKS):
-            square_sums(0, c)
+        square_sums(0, 0)
+        keep_flipped_table(1, tables_flipped)
+        flip_table_back(1)
+        square_sums(0, 1)
         norm_factor(0)
         nc.scalar.copy(out=bias_columns[:], in_=bias_in_psum[:])
         add_bias_flipped(last_flipped)

@@ -343,9 +343,9 @@ def tile_selfattention_pa_s_kernel(tc, x, freqs, w_words, w_scales, b, g, out):
         multiply(nc.vector, 1, 0, 0)
         multiply(nc.vector, 1, 0, 1)
         add_products(nc.gpsimd, 1, 0)
-        add_products(nc.gpsimd, 1, 1)
         multiply(nc.vector, 1, last, 0, in_psum=False, values=last_values)
         multiply(nc.vector, 1, last, 1, in_psum=False, values=last_values)
+        add_products(nc.vector, 1, 1)
         add_products(nc.vector, 1, 2)
         add_products(nc.vector, 1, 3)
         for piece in range(FEATURES // PIECE):

@@ -31,7 +31,6 @@ PIECE_HEADS = 2
 PIECE = PIECE_HEADS * HEAD
 
 WARM_MATMULS = 3
-WARM_TRANSPOSES = 4
 
 FLOPS = 2 * TOKENS * FEATURES * FEATURES
 
@@ -53,10 +52,10 @@ def tile_selfattention_pa_s_kernel(tc, x, freqs, w_words, w_scales, b, g, out):
         g_row = keep.tile([P, HEAD], BF16)
         nc.gpsimd.memset(g_row[:].bitcast(F32), 0.0)
         b_row = keep.tile([P, FEATURES], BF16)
-        nc.vector.memset(b_row[:].bitcast(F32), 0.0)
+        nc.gpsimd.memset(b_row[:].bitcast(F32), 0.0)
+        nc.gpsimd.dma_start(out=b_row[0:1, :], in_=b.rearrange("(o n) -> o n", o=1))
         ident = keep.tile([P, P], F32)
         make_identity(nc, ident[:])
-        nc.gpsimd.dma_start(out=b_row[0:1, :], in_=b.rearrange("(o n) -> o n", o=1))
         w_planes = keep.tile([P, PASSES, FEATURES], U8, align_bytes=64)
         nc.vector.memset(w_planes[:].rearrange("p g n -> p (g n)").bitcast(I32), 0)
 
@@ -76,11 +75,13 @@ def tile_selfattention_pa_s_kernel(tc, x, freqs, w_words, w_scales, b, g, out):
             out=w_sb[:].bitcast(I32), in_=w_words.bitcast(I32).rearrange("g p n -> p g n")
         )
 
+        warm_square = keep.tile([P, P], F32)
+        nc.vector.memset(warm_square[:], 1.0)
         idle_bank = psum_acc.tile([P, BANK], F32, name="acc")
         for i in range(WARM_MATMULS):
-            nc.tensor.matmul(idle_bank[:, 0:P], lhsT=ident[:], rhs=ident[:], start=True, stop=True)
-        for i in range(WARM_TRANSPOSES):
-            nc.tensor.transpose(idle_bank[:, 0:P], ident[:], ident[:])
+            nc.tensor.matmul(
+                idle_bank[:, 0:P], lhsT=warm_square[:], rhs=warm_square[:], start=True, stop=True
+            )
         ones = keep.tile([P, P], BF16)
         nc.vector.memset(ones[:], 1.0)
         one_col = keep.tile([P, 1], F32)

@@ -43,9 +43,8 @@ def tile_selfattention_pa_s_kernel(tc, x, freqs, w_words, w_scales, b, g, out):
 
     with ExitStack() as ctx:
         keep = ctx.enter_context(tc.tile_pool(name="keep", bufs=1))
-        work = ctx.enter_context(tc.tile_pool(name="work", bufs=TOKEN_TILES))
-        psum_short = ctx.enter_context(tc.psum_pool(name="psum_short", bufs=4))
-        psum_table = ctx.enter_context(tc.psum_pool(name="psum_table", bufs=TOKEN_TILES))
+        psum_short = ctx.enter_context(tc.psum_pool(name="psum_short", bufs=5))
+        psum_table = ctx.enter_context(tc.psum_pool(name="psum_table", bufs=1))
         psum_acc = ctx.enter_context(tc.psum_pool(name="psum_acc", bufs=CHUNKS))
         ctx.enter_context(tc.manual_schedule())
 
@@ -86,6 +85,9 @@ def tile_selfattention_pa_s_kernel(tc, x, freqs, w_words, w_scales, b, g, out):
         nc.vector.memset(ones[:], 1.0)
         one_col = keep.tile([P, 1], F32)
         nc.vector.memset(one_col[:], 1.0)
+        swap = keep.tile([P, P], F32)
+        for c in range(2):
+            nc.vector.tensor_copy(out=swap[:, c:P:2], in_=ident[:, 1 - c : P : 2])
         warm = keep.tile([P, 1], F32)
         nc.scalar.activation(out=warm[:], in_=one_col[:], func=ACT.Abs_reciprocal_sqrt)
 
@@ -144,12 +146,13 @@ def tile_selfattention_pa_s_kernel(tc, x, freqs, w_words, w_scales, b, g, out):
             nc.tensor.matmul(everywhere[:], lhsT=ones[:], rhs=b_row[:, cols], start=True, stop=True)
             nc.scalar.copy(out=bias_all[:, cols], in_=everywhere[:])
 
-        table = [keep.tile([P, 2, HEAD], F32, name="table%d" % t) for t in range(TOKEN_TILES)]
+        table = keep.tile([P, 2, HEAD], F32)
+        table_pair = keep.tile([P, 2, HEAD], F32)
 
-        def scale_table(t, gain):
+        def scale_table(gain):
             nc.vector.tensor_tensor(
-                out=table[t][:].rearrange("p c (j i) -> p c j i", i=2),
-                in0=freq_sb[:, t, :].rearrange("p (j i c) -> p c j i", i=2, c=2),
+                out=table[:].rearrange("p c (j i) -> p c j i", i=2),
+                in0=freq_sb[:, 0, :].rearrange("p (j i c) -> p c j i", i=2, c=2),
                 in1=gain[:, 0:HEAD]
                 .rearrange("p (j c) -> p c j", c=2)
                 .unsqueeze(3)
@@ -157,21 +160,31 @@ def tile_selfattention_pa_s_kernel(tc, x, freqs, w_words, w_scales, b, g, out):
                 op=ALU.mult,
             )
 
+        def scale_table_pair(gain):
+            quads = freq_sb[:, 1, :].rearrange("p (j q) -> p j q", q=4)
+            for which, view in enumerate((quads[:, :, 0:4:3], quads[:, :, 2:0:-1])):
+                nc.vector.tensor_tensor(
+                    out=table_pair[:, which, :].rearrange("p (j c) -> p j c", c=2),
+                    in0=view,
+                    in1=gain[:, 0:HEAD].rearrange("p (j c) -> p j c", c=2),
+                    op=ALU.mult,
+                )
+
         table_flipped = keep.tile([P, TOKEN_TILES, 2, P], F32)
-        table_psum = [
-            psum_table.tile([P, 2, HEAD], F32, name="table_psum") for t in range(TOKEN_TILES)
-        ]
+        table_psum = psum_table.tile([P, 2, HEAD], F32, name="table_psum")
 
         def flip_table(t, flipped):
             for cc in range(2):
-                nc.tensor.transpose(flipped[:, t, cc, :], table[t][:, cc, :], ident[:])
+                nc.tensor.transpose(
+                    flipped[:, t, cc, :], (table, table_pair)[t][:, cc, :], ident[:]
+                )
 
         def keep_flipped_table(t, flipped):
             nc.scalar.copy(out=table_flipped[:, t, :, :], in_=flipped[:, t, :, :])
 
-        def flip_table_back(t):
+        def flip_table_back():
             for cc in range(2):
-                nc.tensor.transpose(table_psum[t][:, cc, :], table_flipped[:, t, cc, :], ident[:])
+                nc.tensor.transpose(table_psum[:, cc, :], table_flipped[:, 0, cc, :], ident[:])
 
         def project(t, c):
             acc = psum_acc.tile([P, BANK], F32, name="acc")
@@ -187,20 +200,18 @@ def tile_selfattention_pa_s_kernel(tc, x, freqs, w_words, w_scales, b, g, out):
                 )
             return acc
 
-        bias_columns = keep.tile([P, CHUNK_HEADS], F32)
-        values_flipped = keep.tile([P, CHUNK_HEADS, P], F32)
+        bias_columns = keep.tile([P, HEADS], F32)
 
-        def bias_to_partitions(c):
-            columns = psum_short.tile([P, CHUNK_HEADS], F32, name="short")
-            for hh in range(CHUNK_HEADS):
-                h = c * CHUNK_HEADS + hh
+        def bias_to_partitions():
+            columns = psum_short.tile([P, HEADS], F32, name="short")
+            for h in range(HEADS):
                 nc.tensor.matmul(
-                    columns[:, hh : hh + 1], lhsT=b_row[:, h * HEAD : (h + 1) * HEAD],
+                    columns[:, h : h + 1], lhsT=b_row[:, h * HEAD : (h + 1) * HEAD],
                     rhs=ones[:, 0:1], start=True, stop=True,
                 )
             return columns
 
-        def project_flipped(t, c):
+        def project_flipped(c):
             flipped = psum_short.tile([P, CHUNK_HEADS, P], F32, name="short")
             for hh in range(CHUNK_HEADS):
                 h = c * CHUNK_HEADS + hh
@@ -209,97 +220,131 @@ def tile_selfattention_pa_s_kernel(tc, x, freqs, w_words, w_scales, b, g, out):
                         out=flipped[:, hh, :],
                         lhsT=w_sb[:, gp, 2 * h * HEAD : 2 * (h + 1) * HEAD].bitcast(FP4X4),
                         lhsT_scale=w_planes[:, gp, h * HEAD : (h + 1) * HEAD],
-                        rhs=x_codes[t][:, gp * P : (gp + 1) * P].bitcast(FP8X4),
-                        rhs_scale=x_planes[t][:, gp * P : (gp + 1) * P],
+                        rhs=x_codes[1][:, gp * P : (gp + 1) * P].bitcast(FP8X4),
+                        rhs_scale=x_planes[1][:, gp * P : (gp + 1) * P],
                         start=(gp == 0),
                         stop=(gp == PASSES - 1),
                     )
             return flipped
 
-        def add_bias_flipped(flipped):
-            for hh in range(CHUNK_HEADS):
-                nc.scalar.activation(
-                    out=values_flipped[:, hh, :], in_=flipped[:, hh, :], func=ACT.Identity,
-                    bias=bias_columns[:, hh : hh + 1],
-                )
+        flipped_squares = keep.tile([P, HEADS, P], F32)
+        flipped_parts = keep.tile([P, HEADS, 2, P], F32)
 
-        def flip_values_back():
-            values = psum_acc.tile([P, BANK], F32, name="acc")
-            for hh in range(CHUNK_HEADS):
-                nc.tensor.transpose(
-                    values[:, hh * HEAD : (hh + 1) * HEAD], values_flipped[:, hh, :], ident[:]
-                )
-            return values
-
-        shape = [P, CHUNK_HEADS, PAIRS, 2]
-        u = [work.tile([P, CHUNKS, BANK], F32, name="u") for t in range(TOKEN_TILES)]
-        squares = [work.tile([P, CHUNKS, BANK], F32, name="squares") for t in range(TOKEN_TILES)]
-        sums = [work.tile([P, HEADS], F32, name="sums") for t in range(TOKEN_TILES)]
-        rstd = [work.tile([P, HEADS], F32, name="rstd") for t in range(TOKEN_TILES)]
-        parts = [
-            [work.tile([P, FEATURES], F32, name="part%d" % cc) for cc in range(2)]
-            for t in range(TOKEN_TILES)
-        ]
-        rotated = [work.tile([P, FEATURES], F32, name="rotated") for t in range(TOKEN_TILES)]
-        result = [work.tile([P, FEATURES], F32, name="result") for t in range(TOKEN_TILES)]
-
-        def add_bias(t, c, acc):
-            nc.vector.tensor_tensor(
-                out=u[t][:, c, :], in0=acc[:], in1=bias_all[:, c * BANK : (c + 1) * BANK],
-                op=ALU.add,
-            )
-
-        def square_sums(t, c, values=None):
-            chunk = u[t][:, c, :] if values is None else values[:]
+        def square_flipped(c, flipped):
             for hh in range(CHUNK_HEADS):
                 h = c * CHUNK_HEADS + hh
                 nc.scalar.activation(
-                    out=squares[t][:, c, hh * HEAD : (hh + 1) * HEAD],
-                    in_=chunk[:, hh * HEAD : (hh + 1) * HEAD],
-                    func=ACT.Square,
-                    accum_out=sums[t][:, h : h + 1],
+                    out=flipped_squares[:, h, :], in_=flipped[:, hh, :], func=ACT.Square,
+                    bias=bias_columns[:, h : h + 1],
                 )
 
-        def norm_factor(t):
+        def multiply_flipped(c, flipped):
+            for hh in range(CHUNK_HEADS):
+                h = c * CHUNK_HEADS + hh
+                nc.vector.scalar_tensor_tensor(
+                    out=flipped_parts[:, h, :, :],
+                    in0=flipped[:, hh, :].unsqueeze(1).to_broadcast([P, 2, P]),
+                    scalar=bias_columns[:, h : h + 1],
+                    in1=table_flipped[:, 1, :, :],
+                    op0=ALU.add,
+                    op1=ALU.mult,
+                )
+
+        def sum_squares_flipped(c):
+            sums_bank = psum_short.tile([P, CHUNK_HEADS], F32, name="short")
+            for hh in range(CHUNK_HEADS):
+                nc.tensor.matmul(
+                    sums_bank[:, hh : hh + 1], lhsT=flipped_squares[:, c * CHUNK_HEADS + hh, :],
+                    rhs=warm_square[:, 0:1], start=True, stop=True,
+                )
+            return sums_bank
+
+        def flip_parts_back(piece):
+            values = psum_acc.tile([P, PIECE], F32, name="acc")
+            for i in range(PIECE_HEADS):
+                for which, order in enumerate((ident, swap)):
+                    nc.tensor.matmul(
+                        values[:, i * HEAD : (i + 1) * HEAD],
+                        lhsT=flipped_parts[:, piece * PIECE_HEADS + i, which, :], rhs=order[:],
+                        is_transpose=True, start=(which == 0), stop=(which == 1),
+                    )
+            return values
+
+        shape = [P, CHUNK_HEADS, PAIRS, 2]
+        u = keep.tile([P, CHUNKS, BANK], F32)
+        squares = keep.tile([P, CHUNKS, BANK], F32)
+        sums = keep.tile([P, HEADS], F32)
+        rstd = [keep.tile([P, HEADS], F32, name="rstd%d" % t) for t in range(TOKEN_TILES)]
+        parts = [keep.tile([P, FEATURES], F32, name="part%d" % cc) for cc in range(2)]
+        rotated = keep.tile([P, FEATURES], F32)
+        result = [keep.tile([P, FEATURES], F32, name="result%d" % t) for t in range(TOKEN_TILES)]
+
+        def add_bias(c, acc):
+            nc.vector.tensor_tensor(
+                out=u[:, c, :], in0=acc[:], in1=bias_all[:, c * BANK : (c + 1) * BANK],
+                op=ALU.add,
+            )
+
+        def square_sums(c):
+            for hh in range(CHUNK_HEADS):
+                h = c * CHUNK_HEADS + hh
+                nc.scalar.activation(
+                    out=squares[:, c, hh * HEAD : (hh + 1) * HEAD],
+                    in_=u[:, c, hh * HEAD : (hh + 1) * HEAD],
+                    func=ACT.Square,
+                    accum_out=sums[:, h : h + 1],
+                )
+
+        def norm_factor(t, heads, source):
             nc.scalar.activation(
-                out=rstd[t][:], in_=sums[t][:], func=ACT.Abs_reciprocal_sqrt,
+                out=rstd[t][:, heads], in_=source[:], func=ACT.Abs_reciprocal_sqrt,
                 scale=1.0 / HEAD, bias=EPS,
             )
 
-        def multiply(engine, t, c, cc, in_psum=True, values=None):
-            factors = table_psum[t][:, cc, :] if in_psum else table[t][:, cc, :]
+        def multiply(engine, c, cc, in_psum=True):
+            factors = table_psum[:, cc, :] if in_psum else table[:, cc, :]
             engine.tensor_tensor(
-                out=parts[t][cc][:, c * BANK : (c + 1) * BANK]
+                out=parts[cc][:, c * BANK : (c + 1) * BANK]
                 .rearrange("p (h j i) -> p h j i", h=CHUNK_HEADS, i=2),
-                in0=(u[t][:, c, :] if values is None else values[:])
+                in0=u[:, c, :]
                 .rearrange("p (h j c) -> p h j c", h=CHUNK_HEADS, c=2)[:, :, :, cc : cc + 1]
                 .to_broadcast(shape),
                 in1=factors.rearrange("p (j i) -> p j i", i=2).unsqueeze(1).to_broadcast(shape),
                 op=ALU.mult,
             )
 
-        def add_products(engine, t, piece, pieces=1):
-            cols = slice(piece * PIECE, (piece + pieces) * PIECE)
+        def add_products(engine, c):
+            cols = slice(c * BANK, (c + 1) * BANK)
             engine.tensor_tensor(
-                out=rotated[t][:, cols], in0=parts[t][0][:, cols], in1=parts[t][1][:, cols],
-                op=ALU.add,
+                out=rotated[:, cols], in0=parts[0][:, cols], in1=parts[1][:, cols], op=ALU.add,
             )
 
-        def scale_and_store(t, piece):
+        def scale_and_store(t, piece, source, offset):
             for h in range(piece * PIECE_HEADS, (piece + 1) * PIECE_HEADS):
                 nc.scalar.activation(
                     out=result[t][:, h * HEAD : (h + 1) * HEAD],
-                    in_=rotated[t][:, h * HEAD : (h + 1) * HEAD],
+                    in_=source[:, h * HEAD - offset : (h + 1) * HEAD - offset],
                     func=ACT.Copy,
                     scale=rstd[t][:, h : h + 1],
                 )
             cols = slice(piece * PIECE, (piece + 1) * PIECE)
             nc.sync.dma_start(out=out_rows[t * P : (t + 1) * P, cols], in_=result[t][:, cols])
 
+        def scale_and_store_vector(piece, values):
+            cols = slice(piece * PIECE, (piece + 1) * PIECE)
+            nc.vector.tensor_tensor(
+                out=result[1][:, cols].rearrange("p (h d) -> p h d", d=HEAD),
+                in0=values[:].rearrange("p (h d) -> p h d", d=HEAD),
+                in1=rstd[1][:, piece * PIECE_HEADS : (piece + 1) * PIECE_HEADS]
+                .unsqueeze(2).to_broadcast([P, PIECE_HEADS, HEAD]),
+                op=ALU.mult,
+            )
+            nc.sync.dma_start(out=out_rows[P : 2 * P, cols], in_=result[1][:, cols])
+
         gain = spread_gain()
         banks_of = [transpose_tokens(0)]
-        for t in range(TOKEN_TILES):
-            scale_table(t, gain)
+        scale_table(gain)
+        scale_table_pair(gain)
         banks_of.append(transpose_tokens(1))
         for t in range(TOKEN_TILES):
             regroup_tokens(t, banks_of[t])
@@ -311,43 +356,39 @@ def tile_selfattention_pa_s_kernel(tc, x, freqs, w_words, w_scales, b, g, out):
         first_sums = [project(0, 0)]
         spread_bias(1)
         first_sums.append(project(0, 1))
-        flip_table_back(0)
+        flip_table_back()
         flip_table(1, tables_flipped)
-        for c in range(CHUNKS):
-            add_bias(0, c, first_sums[c])
-        last = CHUNKS - 1
-        second_sums = project(1, 0)
-        bias_in_psum = bias_to_partitions(last)
-        last_flipped = project_flipped(1, last)
-        square_sums(0, 0)
+        bias_in_psum = bias_to_partitions()
         keep_flipped_table(1, tables_flipped)
-        flip_table_back(1)
-        square_sums(0, 1)
-        norm_factor(0)
         nc.scalar.copy(out=bias_columns[:], in_=bias_in_psum[:])
-        add_bias_flipped(last_flipped)
-        last_values = flip_values_back()
-        multiply(nc.gpsimd, 0, 0, 1, in_psum=False)
-        multiply(nc.vector, 0, 0, 0)
-        add_products(nc.gpsimd, 0, 0, 2)
-        multiply(nc.vector, 0, 1, 0)
-        multiply(nc.vector, 0, 1, 1)
-        add_products(nc.gpsimd, 0, 2, 2)
-        add_bias(1, 0, second_sums)
-        scale_and_store(0, 0)
-        scale_and_store(0, 1)
-        square_sums(1, last, values=last_values)
-        square_sums(1, 0)
-        norm_factor(1)
-        scale_and_store(0, 2)
-        scale_and_store(0, 3)
-        multiply(nc.vector, 1, 0, 0)
-        multiply(nc.vector, 1, 0, 1)
-        add_products(nc.gpsimd, 1, 0)
-        multiply(nc.vector, 1, last, 0, in_psum=False, values=last_values)
-        multiply(nc.vector, 1, last, 1, in_psum=False, values=last_values)
-        add_products(nc.vector, 1, 1)
-        add_products(nc.vector, 1, 2)
-        add_products(nc.vector, 1, 3)
-        for piece in range(FEATURES // PIECE):
-            scale_and_store(1, piece)
+        for c in range(CHUNKS):
+            add_bias(c, first_sums[c])
+        flipped = [project_flipped(c) for c in range(CHUNKS)]
+        square_sums(0)
+        multiply(nc.gpsimd, 0, 1, in_psum=False)
+        multiply(nc.vector, 0, 0)
+        add_products(nc.gpsimd, 0)
+        square_flipped(0, flipped[0])
+        sums_of = [sum_squares_flipped(0)]
+        square_sums(1)
+        norm_factor(0, slice(0, HEADS), sums)
+        multiply(nc.vector, 1, 0)
+        multiply(nc.vector, 1, 1)
+        add_products(nc.gpsimd, 1)
+        square_flipped(1, flipped[1])
+        multiply_flipped(0, flipped[0])
+        values = [flip_parts_back(0), flip_parts_back(1)]
+        sums_of.append(sum_squares_flipped(1))
+        multiply_flipped(1, flipped[1])
+        scale_and_store(0, 0, rotated, 0)
+        scale_and_store(0, 1, rotated, 0)
+        norm_factor(1, slice(0, CHUNK_HEADS), sums_of[0])
+        for piece in range(2):
+            scale_and_store(1, piece, values[piece], piece * PIECE)
+        scale_and_store(0, 2, rotated, 0)
+        scale_and_store(0, 3, rotated, 0)
+        norm_factor(1, slice(CHUNK_HEADS, HEADS), sums_of[1])
+        values.append(flip_parts_back(2))
+        values.append(flip_parts_back(3))
+        scale_and_store(1, 2, values[2], 2 * PIECE)
+        scale_and_store_vector(3, values[3])

@@ -29,8 +29,11 @@ CHUNK_HEADS = BANK // HEAD
 HEADS = FEATURES // HEAD
 PIECE_HEADS = 2
 PIECE = PIECE_HEADS * HEAD
+FIRST, SECOND = range(TOKEN_TILES)
 
-WARM_MATMULS = 3
+WARM_MIDDLE = 2
+WARM_TAIL = 1
+WARM_HEAD = 4
 
 FLOPS = 2 * TOKENS * FEATURES * FEATURES
 
@@ -48,22 +51,23 @@ def tile_selfattention_pa_s_kernel(tc, x, freqs, w_words, w_scales, b, g, out):
         psum_acc = ctx.enter_context(tc.psum_pool(name="psum_acc", bufs=CHUNKS))
         ctx.enter_context(tc.manual_schedule())
 
-        g_row = keep.tile([P, HEAD], BF16)
-        nc.gpsimd.memset(g_row[:].bitcast(F32), 0.0)
-        b_row = keep.tile([P, FEATURES], BF16)
-        nc.gpsimd.memset(b_row[:].bitcast(F32), 0.0)
-        nc.gpsimd.dma_start(out=b_row[0:1, :], in_=b.rearrange("(o n) -> o n", o=1))
+        rows = keep.tile([P, P], BF16)
+        nc.vector.memset(rows[:].bitcast(F32), 0.0)
+        nc.gpsimd.dma_start(out=rows[HEADS : HEADS + 1, :], in_=g.rearrange("(o n) -> o n", o=1))
         ident = keep.tile([P, P], F32)
         make_identity(nc, ident[:])
+        warm_square = keep.tile([P, P], F32)
+        nc.vector.memset(warm_square[:], 1.0)
         w_planes = keep.tile([P, PASSES, FEATURES], U8, align_bytes=64)
         nc.vector.memset(w_planes[:].rearrange("p g n -> p (g n)").bitcast(I32), 0)
 
         x_sb = keep.tile([P, TOKEN_TILES, FEATURES], BF16)
         freq_sb = keep.tile([P, TOKEN_TILES, 4 * PAIRS], BF16)
+        bias_all = keep.tile([P, FEATURES], BF16)
         w_sb = keep.tile([P, PASSES, 2 * FEATURES], U8, align_bytes=64)
         nc.sync.dma_start(out=x_sb[:], in_=x_rows.rearrange("(t p) k -> p t k", p=P))
-        nc.sync.dma_start(out=g_row[0:1, :], in_=g.rearrange("(o n) -> o n", o=1))
         nc.sync.dma_start(out=freq_sb[:], in_=freq_rows.rearrange("(t p) f -> p t f", p=P))
+        nc.sync.dma_start(out=rows[0:HEADS, :], in_=b.rearrange("(h d) -> h d", d=HEAD))
         scales_by_row = w_scales.bitcast(I32).rearrange("g q n -> q g n")
         for quad in range(4):
             nc.sync.dma_start(
@@ -73,21 +77,24 @@ def tile_selfattention_pa_s_kernel(tc, x, freqs, w_words, w_scales, b, g, out):
         nc.sync.dma_start(
             out=w_sb[:].bitcast(I32), in_=w_words.bitcast(I32).rearrange("g p n -> p g n")
         )
+        nc.sync.dma_start(out=bias_all[:], in_=b.partition_broadcast(P))
 
-        warm_square = keep.tile([P, P], F32)
-        nc.vector.memset(warm_square[:], 1.0)
         idle_bank = psum_acc.tile([P, BANK], F32, name="acc")
-        for i in range(WARM_MATMULS):
-            nc.tensor.matmul(
-                idle_bank[:, 0:P], lhsT=warm_square[:], rhs=warm_square[:], start=True, stop=True
-            )
-        ones = keep.tile([P, P], BF16)
-        nc.vector.memset(ones[:], 1.0)
+
+        def keep_warm(count, bank):
+            for i in range(count):
+                nc.tensor.matmul(
+                    bank[:, 0:P], lhsT=warm_square[:], rhs=warm_square[:], start=True, stop=True
+                )
+
+        keep_warm(WARM_HEAD, idle_bank)
         one_col = keep.tile([P, 1], F32)
         nc.vector.memset(one_col[:], 1.0)
         swap = keep.tile([P, P], F32)
         for c in range(2):
             nc.vector.tensor_copy(out=swap[:, c:P:2], in_=ident[:, 1 - c : P : 2])
+        ident_bf = keep.tile([P, P], BF16)
+        nc.vector.tensor_copy(out=ident_bf[:], in_=ident[:])
         warm = keep.tile([P, 1], F32)
         nc.scalar.activation(out=warm[:], in_=one_col[:], func=ACT.Abs_reciprocal_sqrt)
 
@@ -118,81 +125,69 @@ def tile_selfattention_pa_s_kernel(tc, x, freqs, w_words, w_scales, b, g, out):
             return banks
 
         def regroup_tokens(t, banks):
-            copy_of_pass = [nc.scalar.copy, nc.vector.tensor_copy if t == 0 else nc.scalar.copy]
-            for gp in range(PASSES):
-                copy_of_pass[gp](
+            for gp, copy in enumerate((nc.scalar.copy, nc.vector.tensor_copy)):
+                copy(
                     out=grouped[t][:, gp, :, :].rearrange("p s v -> p (s v)").bitcast(F32)
                     .rearrange("p (s u) -> p s u", u=2),
                     in_=banks[gp][:].rearrange("p u s -> p s u"),
                 )
 
-        def quantise_tokens(t):
+        def quantise_tokens(t, passes):
+            words = slice(passes.start * P, passes.stop * P)
             nc.vector.quantize_mx(
-                out=x_codes[t][:].bitcast(FP8X4),
-                scales=x_planes[t][:],
-                in_=grouped[t][:].rearrange("p g s v -> p (g s v)"),
+                out=x_codes[t][:, words].bitcast(FP8X4),
+                scales=x_planes[t][:, words],
+                in_=grouped[t][:, passes, :, :].rearrange("p g s v -> p (g s v)"),
             )
 
-        def spread_gain():
-            everywhere = psum_short.tile([P, HEAD], F32, name="short")
-            nc.tensor.matmul(everywhere[:], lhsT=ones[:], rhs=g_row[:], start=True, stop=True)
-            return everywhere
+        columns = keep.tile([P, HEADS + 1], F32)
 
-        bias_all = keep.tile([P, FEATURES], BF16)
+        def flip_rows():
+            flipped = psum_short.tile([P, P], BF16, name="short")
+            nc.tensor.transpose(flipped[:], rows[:], ident_bf[:])
+            nc.scalar.copy(out=columns[:], in_=flipped[:, 0 : HEADS + 1])
 
-        def spread_bias(c):
-            cols = slice(c * BANK, (c + 1) * BANK)
-            everywhere = psum_short.tile([P, BANK], BF16, name="short")
-            nc.tensor.matmul(everywhere[:], lhsT=ones[:], rhs=b_row[:, cols], start=True, stop=True)
-            nc.scalar.copy(out=bias_all[:, cols], in_=everywhere[:])
+        tables = keep.tile([P, TOKEN_TILES, 2, HEAD], BF16)
 
-        table = keep.tile([P, 2, HEAD], F32)
-        table_pair = keep.tile([P, 2, HEAD], F32)
-
-        def scale_table(gain):
-            nc.vector.tensor_tensor(
-                out=table[:].rearrange("p c (j i) -> p c j i", i=2),
-                in0=freq_sb[:, 0, :].rearrange("p (j i c) -> p c j i", i=2, c=2),
-                in1=gain[:, 0:HEAD]
-                .rearrange("p (j c) -> p c j", c=2)
-                .unsqueeze(3)
-                .to_broadcast([P, 2, PAIRS, 2]),
-                op=ALU.mult,
-            )
-
-        def scale_table_pair(gain):
-            quads = freq_sb[:, 1, :].rearrange("p (j q) -> p j q", q=4)
-            for which, view in enumerate((quads[:, :, 0:4:3], quads[:, :, 2:0:-1])):
-                nc.vector.tensor_tensor(
-                    out=table_pair[:, which, :].rearrange("p (j c) -> p j c", c=2),
-                    in0=view,
-                    in1=gain[:, 0:HEAD].rearrange("p (j c) -> p j c", c=2),
-                    op=ALU.mult,
+        def regroup_tables():
+            quads = freq_sb[:].rearrange("p t (j q) -> p t j q", q=4)
+            for which, view in enumerate((quads[:, :, :, 0:4:3], quads[:, :, :, 2:0:-1])):
+                nc.vector.tensor_copy(
+                    out=tables[:, :, which, :].rearrange("p t (j c) -> p t j c", c=2), in_=view
                 )
 
         table_flipped = keep.tile([P, TOKEN_TILES, 2, P], F32)
-        table_psum = psum_table.tile([P, 2, HEAD], F32, name="table_psum")
 
-        def flip_table(t, flipped):
-            for cc in range(2):
-                nc.tensor.transpose(
-                    flipped[:, t, cc, :], (table, table_pair)[t][:, cc, :], ident[:]
-                )
+        def flip_tables():
+            flipped = psum_short.tile([P, TOKEN_TILES, 2, P], BF16, name="short")
+            for t in range(TOKEN_TILES):
+                for which in range(2):
+                    nc.tensor.transpose(flipped[:, t, which, :], tables[:, t, which, :], ident_bf[:])
+            return flipped
 
         def keep_flipped_table(t, flipped):
-            nc.scalar.copy(out=table_flipped[:, t, :, :], in_=flipped[:, t, :, :])
+            nc.scalar.activation(
+                out=table_flipped[:, t, :, :], in_=flipped[:, t, :, :], func=ACT.Copy,
+                scale=columns[:, HEADS : HEADS + 1],
+            )
+
+        table_psum = psum_table.tile([P, 2, HEAD], F32, name="table_psum")
+        table_sbuf = keep.tile([P, HEAD], F32)
 
         def flip_table_back():
-            for cc in range(2):
-                nc.tensor.transpose(table_psum[:, cc, :], table_flipped[:, 0, cc, :], ident[:])
+            for which, order in enumerate((ident, swap)):
+                nc.tensor.transpose(table_psum[:, which, :], table_flipped[:, SECOND, which, :], order[:])
 
-        def project(t, c):
+        def keep_table_for_gpsimd():
+            nc.scalar.copy(out=table_sbuf[:], in_=table_psum[:, 0, :])
+
+        def project(c):
             acc = psum_acc.tile([P, BANK], F32, name="acc")
             for gp in range(PASSES):
                 nc.tensor.matmul_mx(
                     out=acc[:],
-                    lhsT=x_codes[t][:, gp * P : (gp + 1) * P].bitcast(FP8X4),
-                    lhsT_scale=x_planes[t][:, gp * P : (gp + 1) * P],
+                    lhsT=x_codes[SECOND][:, gp * P : (gp + 1) * P].bitcast(FP8X4),
+                    lhsT_scale=x_planes[SECOND][:, gp * P : (gp + 1) * P],
                     rhs=w_sb[:, gp, c * 2 * BANK : (c + 1) * 2 * BANK].bitcast(FP4X4),
                     rhs_scale=w_planes[:, gp, c * BANK : (c + 1) * BANK],
                     start=(gp == 0),
@@ -200,28 +195,17 @@ def tile_selfattention_pa_s_kernel(tc, x, freqs, w_words, w_scales, b, g, out):
                 )
             return acc
 
-        bias_columns = keep.tile([P, HEADS], F32)
-
-        def bias_to_partitions():
-            columns = psum_short.tile([P, HEADS], F32, name="short")
-            for h in range(HEADS):
-                nc.tensor.matmul(
-                    columns[:, h : h + 1], lhsT=b_row[:, h * HEAD : (h + 1) * HEAD],
-                    rhs=ones[:, 0:1], start=True, stop=True,
-                )
-            return columns
-
-        def project_flipped(c):
-            flipped = psum_short.tile([P, CHUNK_HEADS, P], F32, name="short")
-            for hh in range(CHUNK_HEADS):
-                h = c * CHUNK_HEADS + hh
+        def project_flipped(piece):
+            flipped = psum_short.tile([P, PIECE_HEADS, P], F32, name="short")
+            for i in range(PIECE_HEADS):
+                h = piece * PIECE_HEADS + i
                 for gp in range(PASSES):
                     nc.tensor.matmul_mx(
-                        out=flipped[:, hh, :],
+                        out=flipped[:, i, :],
                         lhsT=w_sb[:, gp, 2 * h * HEAD : 2 * (h + 1) * HEAD].bitcast(FP4X4),
                         lhsT_scale=w_planes[:, gp, h * HEAD : (h + 1) * HEAD],
-                        rhs=x_codes[1][:, gp * P : (gp + 1) * P].bitcast(FP8X4),
-                        rhs_scale=x_planes[1][:, gp * P : (gp + 1) * P],
+                        rhs=x_codes[FIRST][:, gp * P : (gp + 1) * P].bitcast(FP8X4),
+                        rhs_scale=x_planes[FIRST][:, gp * P : (gp + 1) * P],
                         start=(gp == 0),
                         stop=(gp == PASSES - 1),
                     )
@@ -230,22 +214,22 @@ def tile_selfattention_pa_s_kernel(tc, x, freqs, w_words, w_scales, b, g, out):
         flipped_squares = keep.tile([P, HEADS, P], F32)
         flipped_parts = keep.tile([P, HEADS, 2, P], F32)
 
-        def square_flipped(c, flipped):
-            for hh in range(CHUNK_HEADS):
-                h = c * CHUNK_HEADS + hh
+        def square_flipped(piece, flipped):
+            for i in range(PIECE_HEADS):
+                h = piece * PIECE_HEADS + i
                 nc.scalar.activation(
-                    out=flipped_squares[:, h, :], in_=flipped[:, hh, :], func=ACT.Square,
-                    bias=bias_columns[:, h : h + 1],
+                    out=flipped_squares[:, h, :], in_=flipped[:, i, :], func=ACT.Square,
+                    bias=columns[:, h : h + 1],
                 )
 
-        def multiply_flipped(c, flipped):
-            for hh in range(CHUNK_HEADS):
-                h = c * CHUNK_HEADS + hh
+        def multiply_flipped(piece, flipped):
+            for i in range(PIECE_HEADS):
+                h = piece * PIECE_HEADS + i
                 nc.vector.scalar_tensor_tensor(
                     out=flipped_parts[:, h, :, :],
-                    in0=flipped[:, hh, :].unsqueeze(1).to_broadcast([P, 2, P]),
-                    scalar=bias_columns[:, h : h + 1],
-                    in1=table_flipped[:, 1, :, :],
+                    in0=flipped[:, i, :].unsqueeze(1).to_broadcast([P, 2, P]),
+                    scalar=columns[:, h : h + 1],
+                    in1=table_flipped[:, FIRST, :, :],
                     op0=ALU.add,
                     op1=ALU.mult,
                 )
@@ -255,17 +239,17 @@ def tile_selfattention_pa_s_kernel(tc, x, freqs, w_words, w_scales, b, g, out):
             for hh in range(CHUNK_HEADS):
                 nc.tensor.matmul(
                     sums_bank[:, hh : hh + 1], lhsT=flipped_squares[:, c * CHUNK_HEADS + hh, :],
-                    rhs=warm_square[:, 0:1], start=True, stop=True,
+                    rhs=one_col[:], start=True, stop=True,
                 )
             return sums_bank
 
-        def flip_parts_back(piece):
-            values = psum_acc.tile([P, PIECE], F32, name="acc")
-            for i in range(PIECE_HEADS):
+        def flip_parts_back(c):
+            values = psum_short.tile([P, BANK], F32, name="short")
+            for hh in range(CHUNK_HEADS):
                 for which, order in enumerate((ident, swap)):
                     nc.tensor.matmul(
-                        values[:, i * HEAD : (i + 1) * HEAD],
-                        lhsT=flipped_parts[:, piece * PIECE_HEADS + i, which, :], rhs=order[:],
+                        values[:, hh * HEAD : (hh + 1) * HEAD],
+                        lhsT=flipped_parts[:, c * CHUNK_HEADS + hh, which, :], rhs=order[:],
                         is_transpose=True, start=(which == 0), stop=(which == 1),
                     )
             return values
@@ -301,14 +285,13 @@ def tile_selfattention_pa_s_kernel(tc, x, freqs, w_words, w_scales, b, g, out):
                 scale=1.0 / HEAD, bias=EPS,
             )
 
-        def multiply(engine, c, cc, in_psum=True):
-            factors = table_psum[:, cc, :] if in_psum else table[:, cc, :]
+        def multiply(engine, c, which, in_psum=True):
+            values = u[:, c, :].rearrange("p (h j c) -> p h j c", h=CHUNK_HEADS, c=2)
+            factors = table_psum[:, which, :] if in_psum else table_sbuf[:]
             engine.tensor_tensor(
-                out=parts[cc][:, c * BANK : (c + 1) * BANK]
+                out=parts[which][:, c * BANK : (c + 1) * BANK]
                 .rearrange("p (h j i) -> p h j i", h=CHUNK_HEADS, i=2),
-                in0=u[:, c, :]
-                .rearrange("p (h j c) -> p h j c", h=CHUNK_HEADS, c=2)[:, :, :, cc : cc + 1]
-                .to_broadcast(shape),
+                in0=values[:, :, :, ::-1] if which else values,
                 in1=factors.rearrange("p (j i) -> p j i", i=2).unsqueeze(1).to_broadcast(shape),
                 op=ALU.mult,
             )
@@ -330,65 +313,70 @@ def tile_selfattention_pa_s_kernel(tc, x, freqs, w_words, w_scales, b, g, out):
             cols = slice(piece * PIECE, (piece + 1) * PIECE)
             nc.sync.dma_start(out=out_rows[t * P : (t + 1) * P, cols], in_=result[t][:, cols])
 
-        def scale_and_store_vector(piece, values):
+        def scale_and_store_by(engine, t, piece, source, offset):
             cols = slice(piece * PIECE, (piece + 1) * PIECE)
-            nc.vector.tensor_tensor(
-                out=result[1][:, cols].rearrange("p (h d) -> p h d", d=HEAD),
-                in0=values[:].rearrange("p (h d) -> p h d", d=HEAD),
-                in1=rstd[1][:, piece * PIECE_HEADS : (piece + 1) * PIECE_HEADS]
+            engine.tensor_tensor(
+                out=result[t][:, cols].rearrange("p (h d) -> p h d", d=HEAD),
+                in0=source[:, cols.start - offset : cols.stop - offset]
+                .rearrange("p (h d) -> p h d", d=HEAD),
+                in1=rstd[t][:, piece * PIECE_HEADS : (piece + 1) * PIECE_HEADS]
                 .unsqueeze(2).to_broadcast([P, PIECE_HEADS, HEAD]),
                 op=ALU.mult,
             )
-            nc.sync.dma_start(out=out_rows[P : 2 * P, cols], in_=result[1][:, cols])
+            nc.sync.dma_start(out=out_rows[t * P : (t + 1) * P, cols], in_=result[t][:, cols])
 
-        gain = spread_gain()
-        banks_of = [transpose_tokens(0)]
-        scale_table(gain)
-        scale_table_pair(gain)
-        banks_of.append(transpose_tokens(1))
+        banks_of = [transpose_tokens(t) for t in range(TOKEN_TILES)]
+        regroup_tables()
+        regroup_tokens(FIRST, banks_of[FIRST])
+        for gp in range(PASSES):
+            quantise_tokens(FIRST, slice(gp, gp + 1))
+        regroup_tokens(SECOND, banks_of[SECOND])
+        quantise_tokens(SECOND, slice(0, PASSES))
+        keep_warm(WARM_MIDDLE, idle_bank)
+        tables_flipped = flip_tables()
+        flip_rows()
         for t in range(TOKEN_TILES):
-            regroup_tokens(t, banks_of[t])
-            quantise_tokens(t)
-        spread_bias(0)
-        tables_flipped = psum_short.tile([P, TOKEN_TILES, 2, P], F32, name="short")
-        flip_table(0, tables_flipped)
-        keep_flipped_table(0, tables_flipped)
-        first_sums = [project(0, 0)]
-        spread_bias(1)
-        first_sums.append(project(0, 1))
+            keep_flipped_table(t, tables_flipped)
+        flipped = [project_flipped(piece) for piece in range(4)]
+        acc = [project(0)]
+        acc.append(project(1))
         flip_table_back()
-        flip_table(1, tables_flipped)
-        bias_in_psum = bias_to_partitions()
-        keep_flipped_table(1, tables_flipped)
-        nc.scalar.copy(out=bias_columns[:], in_=bias_in_psum[:])
-        for c in range(CHUNKS):
-            add_bias(c, first_sums[c])
-        flipped = [project_flipped(c) for c in range(CHUNKS)]
-        square_sums(0)
-        multiply(nc.gpsimd, 0, 1, in_psum=False)
-        multiply(nc.vector, 0, 0)
-        add_products(nc.gpsimd, 0)
-        square_flipped(0, flipped[0])
-        sums_of = [sum_squares_flipped(0)]
-        square_sums(1)
-        norm_factor(0, slice(0, HEADS), sums)
-        multiply(nc.vector, 1, 0)
-        multiply(nc.vector, 1, 1)
-        add_products(nc.gpsimd, 1)
         square_flipped(1, flipped[1])
         multiply_flipped(0, flipped[0])
-        values = [flip_parts_back(0), flip_parts_back(1)]
-        sums_of.append(sum_squares_flipped(1))
+        square_flipped(0, flipped[0])
         multiply_flipped(1, flipped[1])
-        scale_and_store(0, 0, rotated, 0)
-        scale_and_store(0, 1, rotated, 0)
-        norm_factor(1, slice(0, CHUNK_HEADS), sums_of[0])
-        for piece in range(2):
-            scale_and_store(1, piece, values[piece], piece * PIECE)
-        scale_and_store(0, 2, rotated, 0)
-        scale_and_store(0, 3, rotated, 0)
-        norm_factor(1, slice(CHUNK_HEADS, HEADS), sums_of[1])
-        values.append(flip_parts_back(2))
-        values.append(flip_parts_back(3))
-        scale_and_store(1, 2, values[2], 2 * PIECE)
-        scale_and_store_vector(3, values[3])
+        square_flipped(2, flipped[2])
+        multiply_flipped(2, flipped[2])
+        square_flipped(3, flipped[3])
+        keep_table_for_gpsimd()
+        tail_bank = psum_short.tile([P, BANK], F32, name="short")
+        keep_warm(WARM_TAIL, tail_bank)
+        sums_of = [sum_squares_flipped(0)]
+        add_bias(0, acc[0])
+        keep_warm(WARM_TAIL, tail_bank)
+        values = [flip_parts_back(0)]
+        multiply(nc.gpsimd, 0, 0, in_psum=False)
+        multiply_flipped(3, flipped[3])
+        keep_warm(WARM_TAIL, tail_bank)
+        sums_of.append(sum_squares_flipped(1))
+        keep_warm(WARM_TAIL, tail_bank)
+        values.append(flip_parts_back(1))
+        add_bias(1, acc[1])
+        square_sums(0)
+        norm_factor(FIRST, slice(0, CHUNK_HEADS), sums_of[0])
+        scale_and_store(FIRST, 0, values[0], 0)
+        scale_and_store(FIRST, 1, values[0], 0)
+        multiply(nc.vector, 0, 1)
+        add_products(nc.gpsimd, 0)
+        square_sums(1)
+        norm_factor(FIRST, slice(CHUNK_HEADS, HEADS), sums_of[1])
+        norm_factor(SECOND, slice(0, HEADS), sums)
+        multiply(nc.vector, 1, 0)
+        multiply(nc.vector, 1, 1)
+        add_products(nc.vector, 1)
+        scale_and_store(FIRST, 2, values[1], BANK)
+        scale_and_store(FIRST, 3, values[1], BANK)
+        scale_and_store_by(nc.vector, SECOND, 2, rotated, 0)
+        scale_and_store(SECOND, 0, rotated, 0)
+        scale_and_store(SECOND, 1, rotated, 0)
+        scale_and_store_by(nc.vector, SECOND, 3, rotated, 0)

@@ -31,8 +31,7 @@ PIECE_HEADS = 2
 PIECE = PIECE_HEADS * HEAD
 FIRST, SECOND = range(TOKEN_TILES)
 
-WARM_MIDDLE = 2
-WARM_TAIL = 1
+WARM_MIDDLE = 1
 WARM_HEAD = 4
 
 FLOPS = 2 * TOKENS * FEATURES * FEATURES
@@ -243,16 +242,14 @@ def tile_selfattention_pa_s_kernel(tc, x, freqs, w_words, w_scales, b, g, out):
                 )
             return sums_bank
 
-        def flip_parts_back(c):
-            values = psum_short.tile([P, BANK], F32, name="short")
-            for hh in range(CHUNK_HEADS):
+        def flip_parts_back(heads, values):
+            for h in heads:
                 for which, order in enumerate((ident, swap)):
                     nc.tensor.matmul(
-                        values[:, hh * HEAD : (hh + 1) * HEAD],
-                        lhsT=flipped_parts[:, c * CHUNK_HEADS + hh, which, :], rhs=order[:],
+                        values[:, (h - heads.start) * HEAD : (h - heads.start + 1) * HEAD],
+                        lhsT=flipped_parts[:, h, which, :], rhs=order[:],
                         is_transpose=True, start=(which == 0), stop=(which == 1),
                     )
-            return values
 
         shape = [P, CHUNK_HEADS, PAIRS, 2]
         u = keep.tile([P, CHUNKS, BANK], F32)
@@ -296,8 +293,7 @@ def tile_selfattention_pa_s_kernel(tc, x, freqs, w_words, w_scales, b, g, out):
                 op=ALU.mult,
             )
 
-        def add_products(engine, c):
-            cols = slice(c * BANK, (c + 1) * BANK)
+        def add_products(engine, cols):
             engine.tensor_tensor(
                 out=rotated[:, cols], in0=parts[0][:, cols], in1=parts[1][:, cols], op=ALU.add,
             )
@@ -337,46 +333,43 @@ def tile_selfattention_pa_s_kernel(tc, x, freqs, w_words, w_scales, b, g, out):
         flip_rows()
         for t in range(TOKEN_TILES):
             keep_flipped_table(t, tables_flipped)
-        flipped = [project_flipped(piece) for piece in range(4)]
+        flipped = [project_flipped(piece) for piece in range(2)]
         acc = [project(0)]
-        acc.append(project(1))
         flip_table_back()
+        acc.append(project(1))
         square_flipped(1, flipped[1])
         multiply_flipped(0, flipped[0])
         square_flipped(0, flipped[0])
-        multiply_flipped(1, flipped[1])
-        square_flipped(2, flipped[2])
-        multiply_flipped(2, flipped[2])
-        square_flipped(3, flipped[3])
-        keep_table_for_gpsimd()
-        tail_bank = psum_short.tile([P, BANK], F32, name="short")
-        keep_warm(WARM_TAIL, tail_bank)
-        sums_of = [sum_squares_flipped(0)]
         add_bias(0, acc[0])
-        keep_warm(WARM_TAIL, tail_bank)
-        values = [flip_parts_back(0)]
+        keep_table_for_gpsimd()
         multiply(nc.gpsimd, 0, 0, in_psum=False)
-        multiply_flipped(3, flipped[3])
-        keep_warm(WARM_TAIL, tail_bank)
-        sums_of.append(sum_squares_flipped(1))
-        keep_warm(WARM_TAIL, tail_bank)
-        values.append(flip_parts_back(1))
+        multiply_flipped(1, flipped[1])
         add_bias(1, acc[1])
         square_sums(0)
-        norm_factor(FIRST, slice(0, CHUNK_HEADS), sums_of[0])
-        scale_and_store(FIRST, 0, values[0], 0)
-        scale_and_store(FIRST, 1, values[0], 0)
+        sums_of = [sum_squares_flipped(0)]
+        flipped += [project_flipped(piece) for piece in range(2, 4)]
+        values = psum_short.tile([P, BANK], F32, name="short")
+        flip_parts_back(range(0, CHUNK_HEADS), values)
         multiply(nc.vector, 0, 1)
-        add_products(nc.gpsimd, 0)
-        square_sums(1)
-        norm_factor(FIRST, slice(CHUNK_HEADS, HEADS), sums_of[1])
-        norm_factor(SECOND, slice(0, HEADS), sums)
+        add_products(nc.gpsimd, slice(0, BANK))
         multiply(nc.vector, 1, 0)
         multiply(nc.vector, 1, 1)
-        add_products(nc.vector, 1)
-        scale_and_store(FIRST, 2, values[1], BANK)
-        scale_and_store(FIRST, 3, values[1], BANK)
-        scale_and_store_by(nc.vector, SECOND, 2, rotated, 0)
+        add_products(nc.gpsimd, slice(2 * PIECE, 3 * PIECE))
+        square_sums(1)
+        norm_factor(SECOND, slice(0, HEADS), sums)
+        for piece in range(2, 4):
+            square_flipped(piece, flipped[piece])
+            multiply_flipped(piece, flipped[piece])
+        sums_of.append(sum_squares_flipped(1))
+        add_products(nc.vector, slice(3 * PIECE, 4 * PIECE))
+        norm_factor(FIRST, slice(0, CHUNK_HEADS), sums_of[0])
+        scale_and_store(FIRST, 0, values, 0)
+        scale_and_store(FIRST, 1, values, 0)
         scale_and_store(SECOND, 0, rotated, 0)
         scale_and_store(SECOND, 1, rotated, 0)
-        scale_and_store_by(nc.vector, SECOND, 3, rotated, 0)
+        norm_factor(FIRST, slice(CHUNK_HEADS, HEADS), sums_of[1])
+        for piece in range(2, 4):
+            values = psum_acc.tile([P, BANK], F32, name="acc")
+            flip_parts_back(range(piece * PIECE_HEADS, (piece + 1) * PIECE_HEADS), values)
+            scale_and_store_by(nc.vector, FIRST, piece, values, piece * PIECE)
+            scale_and_store(SECOND, piece, rotated, 0)

@@ -31,7 +31,6 @@ PIECE_HEADS = 2
 PIECE = PIECE_HEADS * HEAD
 FIRST, SECOND = range(TOKEN_TILES)
 
-WARM_MIDDLE = 1
 WARM_HEAD = 4
 
 FLOPS = 2 * TOKENS * FEATURES * FEATURES
@@ -50,9 +49,11 @@ def tile_selfattention_pa_s_kernel(tc, x, freqs, w_words, w_scales, b, g, out):
         psum_acc = ctx.enter_context(tc.psum_pool(name="psum_acc", bufs=CHUNKS))
         ctx.enter_context(tc.manual_schedule())
 
-        rows = keep.tile([P, P], BF16)
-        nc.vector.memset(rows[:].bitcast(F32), 0.0)
-        nc.gpsimd.dma_start(out=rows[HEADS : HEADS + 1, :], in_=g.rearrange("(o n) -> o n", o=1))
+        b_rows = keep.tile([P, P], BF16)
+        nc.vector.memset(b_rows[:].bitcast(F32), 0.0)
+        g_row = keep.tile([P, P], BF16)
+        nc.gpsimd.memset(g_row[:].bitcast(F32), 0.0)
+        nc.gpsimd.dma_start(out=g_row[0:1, :], in_=g.rearrange("(o n) -> o n", o=1))
         ident = keep.tile([P, P], F32)
         make_identity(nc, ident[:])
         warm_square = keep.tile([P, P], F32)
@@ -62,11 +63,10 @@ def tile_selfattention_pa_s_kernel(tc, x, freqs, w_words, w_scales, b, g, out):
 
         x_sb = keep.tile([P, TOKEN_TILES, FEATURES], BF16)
         freq_sb = keep.tile([P, TOKEN_TILES, 4 * PAIRS], BF16)
-        bias_all = keep.tile([P, FEATURES], BF16)
         w_sb = keep.tile([P, PASSES, 2 * FEATURES], U8, align_bytes=64)
         nc.sync.dma_start(out=x_sb[:], in_=x_rows.rearrange("(t p) k -> p t k", p=P))
         nc.sync.dma_start(out=freq_sb[:], in_=freq_rows.rearrange("(t p) f -> p t f", p=P))
-        nc.sync.dma_start(out=rows[0:HEADS, :], in_=b.rearrange("(h d) -> h d", d=HEAD))
+        nc.sync.dma_start(out=b_rows[0:HEADS, :], in_=b.rearrange("(h d) -> h d", d=HEAD))
         scales_by_row = w_scales.bitcast(I32).rearrange("g q n -> q g n")
         for quad in range(4):
             nc.sync.dma_start(
@@ -76,7 +76,6 @@ def tile_selfattention_pa_s_kernel(tc, x, freqs, w_words, w_scales, b, g, out):
         nc.sync.dma_start(
             out=w_sb[:].bitcast(I32), in_=w_words.bitcast(I32).rearrange("g p n -> p g n")
         )
-        nc.sync.dma_start(out=bias_all[:], in_=b.partition_broadcast(P))
 
         idle_bank = psum_acc.tile([P, BANK], F32, name="acc")
 
@@ -139,12 +138,23 @@ def tile_selfattention_pa_s_kernel(tc, x, freqs, w_words, w_scales, b, g, out):
                 in_=grouped[t][:, passes, :, :].rearrange("p g s v -> p (g s v)"),
             )
 
-        columns = keep.tile([P, HEADS + 1], F32)
+        columns = keep.tile([P, HEADS], F32)
+        gain = keep.tile([P, 1], F32)
+        bias_all = keep.tile([P, FEATURES], BF16)
 
-        def flip_rows():
-            flipped = psum_short.tile([P, P], BF16, name="short")
-            nc.tensor.transpose(flipped[:], rows[:], ident_bf[:])
-            nc.scalar.copy(out=columns[:], in_=flipped[:, 0 : HEADS + 1])
+        def spread_bias(c):
+            everywhere = psum_short.tile([P, BANK], BF16, name="short")
+            for hh in range(CHUNK_HEADS):
+                h = c * CHUNK_HEADS + hh
+                nc.tensor.matmul(
+                    everywhere[:, hh * HEAD : (hh + 1) * HEAD],
+                    lhsT=ident_bf[:, h : h + 1].to_broadcast([P, P]), rhs=b_rows[:],
+                    start=True, stop=True,
+                )
+            return everywhere
+
+        def keep_bias(copy, c, everywhere):
+            copy(out=bias_all[:, c * BANK : (c + 1) * BANK], in_=everywhere[:])
 
         tables = keep.tile([P, TOKEN_TILES, 2, HEAD], BF16)
 
@@ -157,17 +167,23 @@ def tile_selfattention_pa_s_kernel(tc, x, freqs, w_words, w_scales, b, g, out):
 
         table_flipped = keep.tile([P, TOKEN_TILES, 2, P], F32)
 
-        def flip_tables():
-            flipped = psum_short.tile([P, TOKEN_TILES, 2, P], BF16, name="short")
+        def flip_small():
+            small = psum_short.tile([P, 6, P], BF16, name="short")
+            nc.tensor.transpose(small[:, 4, :], b_rows[:], ident_bf[:])
             for t in range(TOKEN_TILES):
                 for which in range(2):
-                    nc.tensor.transpose(flipped[:, t, which, :], tables[:, t, which, :], ident_bf[:])
-            return flipped
+                    nc.tensor.transpose(small[:, 2 * t + which, :], tables[:, t, which, :], ident_bf[:])
+            nc.tensor.transpose(small[:, 5, :], g_row[:], ident_bf[:])
+            return small
+
+        def keep_columns(small):
+            nc.scalar.copy(out=columns[:], in_=small[:, 4, 0:HEADS])
+            nc.scalar.copy(out=gain[:], in_=small[:, 5, 0:1])
 
         def keep_flipped_table(t, flipped):
             nc.scalar.activation(
-                out=table_flipped[:, t, :, :], in_=flipped[:, t, :, :], func=ACT.Copy,
-                scale=columns[:, HEADS : HEADS + 1],
+                out=table_flipped[:, t, :, :], in_=flipped[:, 2 * t : 2 * t + 2, :], func=ACT.Copy,
+                scale=gain[:],
             )
 
         table_psum = psum_table.tile([P, 2, HEAD], F32, name="table_psum")
@@ -326,13 +342,14 @@ def tile_selfattention_pa_s_kernel(tc, x, freqs, w_words, w_scales, b, g, out):
         regroup_tokens(FIRST, banks_of[FIRST])
         for gp in range(PASSES):
             quantise_tokens(FIRST, slice(gp, gp + 1))
+        everywhere = [spread_bias(c) for c in range(CHUNKS)]
         regroup_tokens(SECOND, banks_of[SECOND])
+        keep_bias(nc.vector.tensor_copy, 0, everywhere[0])
         quantise_tokens(SECOND, slice(0, PASSES))
-        keep_warm(WARM_MIDDLE, idle_bank)
-        tables_flipped = flip_tables()
-        flip_rows()
+        small = flip_small()
+        keep_columns(small)
         for t in range(TOKEN_TILES):
-            keep_flipped_table(t, tables_flipped)
+            keep_flipped_table(t, small)
         flipped = [project_flipped(piece) for piece in range(2)]
         acc = [project(0)]
         flip_table_back()
@@ -342,6 +359,7 @@ def tile_selfattention_pa_s_kernel(tc, x, freqs, w_words, w_scales, b, g, out):
         square_flipped(0, flipped[0])
         add_bias(0, acc[0])
         keep_table_for_gpsimd()
+        keep_bias(nc.scalar.copy, 1, everywhere[1])
         multiply(nc.gpsimd, 0, 0, in_psum=False)
         multiply_flipped(1, flipped[1])
         add_bias(1, acc[1])
@@ -371,5 +389,5 @@ def tile_selfattention_pa_s_kernel(tc, x, freqs, w_words, w_scales, b, g, out):
         for piece in range(2, 4):
             values = psum_acc.tile([P, BANK], F32, name="acc")
             flip_parts_back(range(piece * PIECE_HEADS, (piece + 1) * PIECE_HEADS), values)
-            scale_and_store_by(nc.vector, FIRST, piece, values, piece * PIECE)
             scale_and_store(SECOND, piece, rotated, 0)
+            scale_and_store_by(nc.vector, FIRST, piece, values, piece * PIECE)

@@ -123,7 +123,8 @@ def tile_selfattention_pa_s_kernel(tc, x, freqs, w_words, w_scales, b, g, out):
             return banks
 
         def regroup_tokens(t, banks):
-            for gp, copy in enumerate((nc.scalar.copy, nc.vector.tensor_copy)):
+            copy_of_pass = (nc.scalar.copy, nc.vector.tensor_copy if t == FIRST else nc.scalar.copy)
+            for gp, copy in enumerate(copy_of_pass):
                 copy(
                     out=grouped[t][:, gp, :, :].rearrange("p s v -> p (s v)").bitcast(F32)
                     .rearrange("p (s u) -> p s u", u=2),
@@ -177,8 +178,8 @@ def tile_selfattention_pa_s_kernel(tc, x, freqs, w_words, w_scales, b, g, out):
             return small
 
         def keep_columns(small):
-            nc.scalar.copy(out=columns[:], in_=small[:, 4, 0:HEADS])
             nc.scalar.copy(out=gain[:], in_=small[:, 5, 0:1])
+            nc.scalar.copy(out=columns[:], in_=small[:, 4, 0:HEADS])
 
         def keep_flipped_table(t, flipped):
             nc.scalar.activation(
@@ -342,30 +343,31 @@ def tile_selfattention_pa_s_kernel(tc, x, freqs, w_words, w_scales, b, g, out):
         regroup_tokens(FIRST, banks_of[FIRST])
         for gp in range(PASSES):
             quantise_tokens(FIRST, slice(gp, gp + 1))
-        everywhere = [spread_bias(c) for c in range(CHUNKS)]
+        everywhere = [spread_bias(0)]
         regroup_tokens(SECOND, banks_of[SECOND])
-        keep_bias(nc.vector.tensor_copy, 0, everywhere[0])
         quantise_tokens(SECOND, slice(0, PASSES))
+        keep_bias(nc.vector.tensor_copy, 0, everywhere[0])
         small = flip_small()
         keep_columns(small)
         for t in range(TOKEN_TILES):
             keep_flipped_table(t, small)
         flipped = [project_flipped(piece) for piece in range(2)]
+        everywhere.append(spread_bias(1))
         acc = [project(0)]
         flip_table_back()
         acc.append(project(1))
         square_flipped(1, flipped[1])
         multiply_flipped(0, flipped[0])
+        keep_bias(nc.scalar.copy, 1, everywhere[1])
         square_flipped(0, flipped[0])
+        multiply_flipped(1, flipped[1])
         add_bias(0, acc[0])
         keep_table_for_gpsimd()
-        keep_bias(nc.scalar.copy, 1, everywhere[1])
         multiply(nc.gpsimd, 0, 0, in_psum=False)
-        multiply_flipped(1, flipped[1])
         add_bias(1, acc[1])
         square_sums(0)
-        sums_of = [sum_squares_flipped(0)]
         flipped += [project_flipped(piece) for piece in range(2, 4)]
+        sums_of = [sum_squares_flipped(0)]
         values = psum_short.tile([P, BANK], F32, name="short")
         flip_parts_back(range(0, CHUNK_HEADS), values)
         multiply(nc.vector, 0, 1)
@@ -373,12 +375,12 @@ def tile_selfattention_pa_s_kernel(tc, x, freqs, w_words, w_scales, b, g, out):
         multiply(nc.vector, 1, 0)
         multiply(nc.vector, 1, 1)
         add_products(nc.gpsimd, slice(2 * PIECE, 3 * PIECE))
-        square_sums(1)
-        norm_factor(SECOND, slice(0, HEADS), sums)
         for piece in range(2, 4):
             square_flipped(piece, flipped[piece])
             multiply_flipped(piece, flipped[piece])
         sums_of.append(sum_squares_flipped(1))
+        square_sums(1)
+        norm_factor(SECOND, slice(0, HEADS), sums)
         add_products(nc.vector, slice(3 * PIECE, 4 * PIECE))
         norm_factor(FIRST, slice(0, CHUNK_HEADS), sums_of[0])
         scale_and_store(FIRST, 0, values, 0)

@@ -63,7 +63,10 @@ def tile_selfattention_pa_s_kernel(tc, x, freqs, w_words, w_scales, b, g, out):
 
         x_sb = keep.tile([P, TOKEN_TILES, FEATURES], BF16)
         freq_sb = keep.tile([P, TOKEN_TILES, 4 * PAIRS], BF16)
-        w_sb = keep.tile([P, PASSES, 2 * FEATURES], U8, align_bytes=64)
+        w_sb = [
+            keep.tile([P, PASSES, 2 * BANK], U8, name="w%d" % c, align_bytes=64)
+            for c in range(CHUNKS)
+        ]
         nc.sync.dma_start(out=x_sb[:], in_=x_rows.rearrange("(t p) k -> p t k", p=P))
         nc.sync.dma_start(out=freq_sb[:], in_=freq_rows.rearrange("(t p) f -> p t f", p=P))
         nc.sync.dma_start(out=b_rows[0:HEADS, :], in_=b.rearrange("(h d) -> h d", d=HEAD))
@@ -73,9 +76,12 @@ def tile_selfattention_pa_s_kernel(tc, x, freqs, w_words, w_scales, b, g, out):
                 out=w_planes[32 * quad : 32 * quad + 4, :, :].bitcast(I32),
                 in_=scales_by_row[4 * quad : 4 * quad + 4, :, :],
             )
-        nc.sync.dma_start(
-            out=w_sb[:].bitcast(I32), in_=w_words.bitcast(I32).rearrange("g p n -> p g n")
-        )
+        w_by_row = w_words.rearrange("g p n -> p g n")
+        for c in range(CHUNKS):
+            nc.sync.dma_start(
+                out=w_sb[c][:].bitcast(I32),
+                in_=w_by_row[:, :, c * 2 * BANK : (c + 1) * 2 * BANK].bitcast(I32),
+            )
 
         idle_bank = psum_acc.tile([P, BANK], F32, name="acc")
 
@@ -204,7 +210,7 @@ def tile_selfattention_pa_s_kernel(tc, x, freqs, w_words, w_scales, b, g, out):
                     out=acc[:],
                     lhsT=x_codes[SECOND][:, gp * P : (gp + 1) * P].bitcast(FP8X4),
                     lhsT_scale=x_planes[SECOND][:, gp * P : (gp + 1) * P],
-                    rhs=w_sb[:, gp, c * 2 * BANK : (c + 1) * 2 * BANK].bitcast(FP4X4),
+                    rhs=w_sb[c][:, gp, :].bitcast(FP4X4),
                     rhs_scale=w_planes[:, gp, c * BANK : (c + 1) * BANK],
                     start=(gp == 0),
                     stop=(gp == PASSES - 1),
@@ -215,10 +221,11 @@ def tile_selfattention_pa_s_kernel(tc, x, freqs, w_words, w_scales, b, g, out):
             flipped = psum_short.tile([P, PIECE_HEADS, P], F32, name="short")
             for i in range(PIECE_HEADS):
                 h = piece * PIECE_HEADS + i
+                hh = h % CHUNK_HEADS
                 for gp in range(PASSES):
                     nc.tensor.matmul_mx(
                         out=flipped[:, i, :],
-                        lhsT=w_sb[:, gp, 2 * h * HEAD : 2 * (h + 1) * HEAD].bitcast(FP4X4),
+                        lhsT=w_sb[h // CHUNK_HEADS][:, gp, 2 * hh * HEAD : 2 * (hh + 1) * HEAD].bitcast(FP4X4),
                         lhsT_scale=w_planes[:, gp, h * HEAD : (h + 1) * HEAD],
                         rhs=x_codes[FIRST][:, gp * P : (gp + 1) * P].bitcast(FP8X4),
                         rhs_scale=x_planes[FIRST][:, gp * P : (gp + 1) * P],
@@ -384,10 +391,10 @@ def tile_selfattention_pa_s_kernel(tc, x, freqs, w_words, w_scales, b, g, out):
         add_products(nc.vector, slice(3 * PIECE, 4 * PIECE))
         norm_factor(FIRST, slice(0, CHUNK_HEADS), sums_of[0])
         scale_and_store(FIRST, 0, values, 0)
+        norm_factor(FIRST, slice(CHUNK_HEADS, HEADS), sums_of[1])
         scale_and_store(FIRST, 1, values, 0)
         scale_and_store(SECOND, 0, rotated, 0)
         scale_and_store(SECOND, 1, rotated, 0)
-        norm_factor(FIRST, slice(CHUNK_HEADS, HEADS), sums_of[1])
         for piece in range(2, 4):
             values = psum_acc.tile([P, BANK], F32, name="acc")
             flip_parts_back(range(piece * PIECE_HEADS, (piece + 1) * PIECE_HEADS), values)

@@ -360,9 +360,8 @@ def tile_selfattention_pa_s_kernel(tc, x, freqs, w_words, w_scales, b, g, out):
             keep_flipped_table(t, small)
         flipped = [project_flipped(piece) for piece in range(2)]
         everywhere.append(spread_bias(1))
-        acc = [project(0)]
+        acc = [project(c) for c in range(CHUNKS)]
         flip_table_back()
-        acc.append(project(1))
         square_flipped(1, flipped[1])
         multiply_flipped(0, flipped[0])
         keep_bias(nc.scalar.copy, 1, everywhere[1])
@@ -386,17 +385,21 @@ def tile_selfattention_pa_s_kernel(tc, x, freqs, w_words, w_scales, b, g, out):
             square_flipped(piece, flipped[piece])
             multiply_flipped(piece, flipped[piece])
         sums_of.append(sum_squares_flipped(1))
-        square_sums(1)
-        norm_factor(SECOND, slice(0, HEADS), sums)
-        add_products(nc.vector, slice(3 * PIECE, 4 * PIECE))
         norm_factor(FIRST, slice(0, CHUNK_HEADS), sums_of[0])
+        square_sums(1)
         scale_and_store(FIRST, 0, values, 0)
-        norm_factor(FIRST, slice(CHUNK_HEADS, HEADS), sums_of[1])
         scale_and_store(FIRST, 1, values, 0)
+        norm_factor(SECOND, slice(0, HEADS), sums)
+        norm_factor(FIRST, slice(CHUNK_HEADS, HEADS), sums_of[1])
         scale_and_store(SECOND, 0, rotated, 0)
         scale_and_store(SECOND, 1, rotated, 0)
         for piece in range(2, 4):
             values = psum_acc.tile([P, BANK], F32, name="acc")
             flip_parts_back(range(piece * PIECE_HEADS, (piece + 1) * PIECE_HEADS), values)
-            scale_and_store(SECOND, piece, rotated, 0)
-            scale_and_store_by(nc.vector, FIRST, piece, values, piece * PIECE)
+            if piece == 2:
+                scale_and_store_by(nc.vector, FIRST, piece, values, piece * PIECE)
+                add_products(nc.vector, slice(3 * PIECE, 4 * PIECE))
+                scale_and_store(SECOND, piece, rotated, 0)
+            else:
+                scale_and_store(FIRST, piece, values, piece * PIECE)
+                scale_and_store_by(nc.vector, SECOND, piece, rotated, 0)

@@ -275,9 +275,8 @@ def tile_selfattention_pa_s_kernel(tc, x, freqs, w_words, w_scales, b, g, out):
                         is_transpose=True, start=(which == 0), stop=(which == 1),
                     )
 
-        shape = [P, CHUNK_HEADS, PAIRS, 2]
-        u = keep.tile([P, CHUNKS, BANK], F32)
-        squares = keep.tile([P, CHUNKS, BANK], F32)
+        u = keep.tile([P, FEATURES], F32)
+        squares = keep.tile([P, FEATURES], F32)
         sums = keep.tile([P, HEADS], F32)
         rstd = [keep.tile([P, HEADS], F32, name="rstd%d" % t) for t in range(TOKEN_TILES)]
         parts = [keep.tile([P, FEATURES], F32, name="part%d" % cc) for cc in range(2)]
@@ -286,7 +285,7 @@ def tile_selfattention_pa_s_kernel(tc, x, freqs, w_words, w_scales, b, g, out):
 
         def add_bias(c, acc):
             nc.vector.tensor_tensor(
-                out=u[:, c, :], in0=acc[:], in1=bias_all[:, c * BANK : (c + 1) * BANK],
+                out=u[:, c * BANK : (c + 1) * BANK], in0=acc[:], in1=bias_all[:, c * BANK : (c + 1) * BANK],
                 op=ALU.add,
             )
 
@@ -294,8 +293,8 @@ def tile_selfattention_pa_s_kernel(tc, x, freqs, w_words, w_scales, b, g, out):
             for hh in range(CHUNK_HEADS):
                 h = c * CHUNK_HEADS + hh
                 nc.scalar.activation(
-                    out=squares[:, c, hh * HEAD : (hh + 1) * HEAD],
-                    in_=u[:, c, hh * HEAD : (hh + 1) * HEAD],
+                    out=squares[:, h * HEAD : (h + 1) * HEAD],
+                    in_=u[:, h * HEAD : (h + 1) * HEAD],
                     func=ACT.Square,
                     accum_out=sums[:, h : h + 1],
                 )
@@ -306,14 +305,16 @@ def tile_selfattention_pa_s_kernel(tc, x, freqs, w_words, w_scales, b, g, out):
                 scale=1.0 / HEAD, bias=EPS,
             )
 
-        def multiply(engine, c, which, in_psum=True):
-            values = u[:, c, :].rearrange("p (h j c) -> p h j c", h=CHUNK_HEADS, c=2)
+        def multiply(engine, pieces, which, in_psum=True):
+            cols = slice(pieces.start * PIECE, pieces.stop * PIECE)
+            heads = len(pieces) * PIECE_HEADS
+            values = u[:, cols].rearrange("p (h j c) -> p h j c", h=heads, c=2)
             factors = table_psum[:, which, :] if in_psum else table_sbuf[:]
             engine.tensor_tensor(
-                out=parts[which][:, c * BANK : (c + 1) * BANK]
-                .rearrange("p (h j i) -> p h j i", h=CHUNK_HEADS, i=2),
+                out=parts[which][:, cols].rearrange("p (h j i) -> p h j i", h=heads, i=2),
                 in0=values[:, :, :, ::-1] if which else values,
-                in1=factors.rearrange("p (j i) -> p j i", i=2).unsqueeze(1).to_broadcast(shape),
+                in1=factors.rearrange("p (j i) -> p j i", i=2).unsqueeze(1)
+                .to_broadcast([P, heads, PAIRS, 2]),
                 op=ALU.mult,
             )
 
@@ -369,21 +370,23 @@ def tile_selfattention_pa_s_kernel(tc, x, freqs, w_words, w_scales, b, g, out):
         multiply_flipped(1, flipped[1])
         add_bias(0, acc[0])
         keep_table_for_gpsimd()
-        multiply(nc.gpsimd, 0, 0, in_psum=False)
+        multiply(nc.gpsimd, range(2), 0, in_psum=False)
         add_bias(1, acc[1])
         square_sums(0)
         flipped += [project_flipped(piece) for piece in range(2, 4)]
         sums_of = [sum_squares_flipped(0)]
         values = psum_short.tile([P, BANK], F32, name="short")
         flip_parts_back(range(0, CHUNK_HEADS), values)
-        multiply(nc.vector, 0, 1)
+        multiply(nc.vector, range(2), 1)
         add_products(nc.gpsimd, slice(0, BANK))
-        multiply(nc.vector, 1, 0)
-        multiply(nc.vector, 1, 1)
+        for which in range(2):
+            multiply(nc.vector, range(2, 3), which)
         add_products(nc.gpsimd, slice(2 * PIECE, 3 * PIECE))
         for piece in range(2, 4):
             square_flipped(piece, flipped[piece])
             multiply_flipped(piece, flipped[piece])
+        for which in range(2):
+            multiply(nc.vector, range(3, 4), which)
         sums_of.append(sum_squares_flipped(1))
         norm_factor(FIRST, slice(0, CHUNK_HEADS), sums_of[0])
         square_sums(1)

@@ -360,25 +360,26 @@ def tile_selfattention_pa_s_kernel(tc, x, freqs, w_words, w_scales, b, g, out):
         for t in range(TOKEN_TILES):
             keep_flipped_table(t, small)
         flipped = [project_flipped(piece) for piece in range(2)]
-        everywhere.append(spread_bias(1))
-        acc = [project(c) for c in range(CHUNKS)]
+        acc = [project(0)]
         flip_table_back()
+        everywhere.append(spread_bias(1))
+        acc.append(project(1))
         square_flipped(1, flipped[1])
         multiply_flipped(0, flipped[0])
-        keep_bias(nc.scalar.copy, 1, everywhere[1])
         square_flipped(0, flipped[0])
-        multiply_flipped(1, flipped[1])
         add_bias(0, acc[0])
         keep_table_for_gpsimd()
+        keep_bias(nc.scalar.copy, 1, everywhere[1])
         multiply(nc.gpsimd, range(2), 0, in_psum=False)
+        multiply_flipped(1, flipped[1])
+        multiply(nc.vector, range(2), 1)
+        add_products(nc.gpsimd, slice(0, BANK))
         add_bias(1, acc[1])
         square_sums(0)
         flipped += [project_flipped(piece) for piece in range(2, 4)]
         sums_of = [sum_squares_flipped(0)]
         values = psum_short.tile([P, BANK], F32, name="short")
         flip_parts_back(range(0, CHUNK_HEADS), values)
-        multiply(nc.vector, range(2), 1)
-        add_products(nc.gpsimd, slice(0, BANK))
         for which in range(2):
             multiply(nc.vector, range(2, 3), which)
         add_products(nc.gpsimd, slice(2 * PIECE, 3 * PIECE))
@@ -393,16 +394,16 @@ def tile_selfattention_pa_s_kernel(tc, x, freqs, w_words, w_scales, b, g, out):
         scale_and_store(FIRST, 0, values, 0)
         scale_and_store(FIRST, 1, values, 0)
         norm_factor(SECOND, slice(0, HEADS), sums)
-        norm_factor(FIRST, slice(CHUNK_HEADS, HEADS), sums_of[1])
         scale_and_store(SECOND, 0, rotated, 0)
+        norm_factor(FIRST, slice(CHUNK_HEADS, HEADS), sums_of[1])
         scale_and_store(SECOND, 1, rotated, 0)
+        add_products(nc.vector, slice(3 * PIECE, 4 * PIECE))
+        values = []
         for piece in range(2, 4):
-            values = psum_acc.tile([P, BANK], F32, name="acc")
-            flip_parts_back(range(piece * PIECE_HEADS, (piece + 1) * PIECE_HEADS), values)
-            if piece == 2:
-                scale_and_store_by(nc.vector, FIRST, piece, values, piece * PIECE)
-                add_products(nc.vector, slice(3 * PIECE, 4 * PIECE))
-                scale_and_store(SECOND, piece, rotated, 0)
-            else:
-                scale_and_store(FIRST, piece, values, piece * PIECE)
-                scale_and_store_by(nc.vector, SECOND, piece, rotated, 0)
+            bank = psum_acc.tile([P, BANK], F32, name="acc")
+            flip_parts_back(range(piece * PIECE_HEADS, (piece + 1) * PIECE_HEADS), bank)
+            values.append(bank)
+        scale_and_store(FIRST, 2, values[0], 2 * PIECE)
+        scale_and_store(SECOND, 2, rotated, 0)
+        scale_and_store_by(nc.vector, FIRST, 3, values[1], 3 * PIECE)
+        scale_and_store(SECOND, 3, rotated, 0)

from contextlib import ExitStack

import concourse.mybir as mybir
from concourse.masks import make_identity

F32 = mybir.dt.float32
BF16 = mybir.dt.bfloat16
I32 = mybir.dt.int32
U32 = mybir.dt.uint32
U8 = mybir.dt.uint8
FP8X4 = mybir.dt.float8_e4m3fn_x4
FP4X4 = mybir.dt.float4_e2m1fn_x4
ACT = mybir.ActivationFunctionType
ALU = mybir.AluOpType

P = 128
TOKENS = 256
FEATURES = 1024
HEAD = 128
PAIRS = HEAD // 2
EPS = 1e-6

K_PASS = 512
PASSES = FEATURES // K_PASS
TOKEN_TILES = TOKENS // P
BANK = 512
CHUNKS = FEATURES // BANK
CHUNK_HEADS = BANK // HEAD
HEADS = FEATURES // HEAD
PIECE_HEADS = 2
PIECE = PIECE_HEADS * HEAD
FIRST, SECOND = range(TOKEN_TILES)

WARM_HEAD = 4

FLOPS = 2 * TOKENS * FEATURES * FEATURES


def tile_selfattention_pa_s_kernel(tc, x, freqs, w_words, w_scales, b, g, out):
    nc = tc.nc
    x_rows = x.flatten_outer_dims()
    freq_rows = freqs.rearrange("a s b j i c -> (a s b) (j i c)")
    out_rows = out.rearrange("a s h d -> (a s) (h d)")

    with ExitStack() as ctx:
        keep = ctx.enter_context(tc.tile_pool(name="keep", bufs=1))
        psum_short = ctx.enter_context(tc.psum_pool(name="psum_short", bufs=5))
        psum_table = ctx.enter_context(tc.psum_pool(name="psum_table", bufs=1))
        psum_acc = ctx.enter_context(tc.psum_pool(name="psum_acc", bufs=CHUNKS))
        ctx.enter_context(tc.manual_schedule())

        b_rows = keep.tile([P, P], BF16)
        nc.vector.memset(b_rows[:].bitcast(F32), 0.0)
        g_row = keep.tile([P, P], BF16)
        nc.gpsimd.memset(g_row[:].bitcast(F32), 0.0)
        nc.gpsimd.dma_start(out=g_row[0:1, :], in_=g.rearrange("(o n) -> o n", o=1))
        ident = keep.tile([P, P], F32)
        make_identity(nc, ident[:])
        warm_square = keep.tile([P, P], F32)
        nc.vector.memset(warm_square[:], 1.0)
        w_planes = keep.tile([P, PASSES, FEATURES], U8, align_bytes=64)
        nc.vector.memset(w_planes[:].rearrange("p g n -> p (g n)").bitcast(I32), 0)

        x_sb = keep.tile([P, TOKEN_TILES, FEATURES], BF16)
        freq_sb = keep.tile([P, TOKEN_TILES, 4 * PAIRS], BF16)
        w_sb = [
            keep.tile([P, PASSES, 2 * BANK], U8, name="w%d" % c, align_bytes=64)
            for c in range(CHUNKS)
        ]
        nc.sync.dma_start(out=x_sb[:], in_=x_rows.rearrange("(t p) k -> p t k", p=P))
        nc.sync.dma_start(out=freq_sb[:], in_=freq_rows.rearrange("(t p) f -> p t f", p=P))
        nc.sync.dma_start(out=b_rows[0:HEADS, :], in_=b.rearrange("(h d) -> h d", d=HEAD))
        scales_by_row = w_scales.bitcast(I32).rearrange("g q n -> q g n")
        for quad in range(4):
            nc.sync.dma_start(
                out=w_planes[32 * quad : 32 * quad + 4, :, :].bitcast(I32),
                in_=scales_by_row[4 * quad : 4 * quad + 4, :, :],
            )
        w_by_row = w_words.rearrange("g p n -> p g n")
        for c in range(CHUNKS):
            nc.sync.dma_start(
                out=w_sb[c][:].bitcast(I32),
                in_=w_by_row[:, :, c * 2 * BANK : (c + 1) * 2 * BANK].bitcast(I32),
            )

        idle_bank = psum_acc.tile([P, BANK], F32, name="acc")

        def keep_warm(count, bank):
            for i in range(count):
                nc.tensor.matmul(
                    bank[:, 0:P], lhsT=warm_square[:], rhs=warm_square[:], start=True, stop=True
                )

        keep_warm(WARM_HEAD, idle_bank)
        one_col = keep.tile([P, 1], F32)
        nc.vector.memset(one_col[:], 1.0)
        swap = keep.tile([P, P], F32)
        for c in range(2):
            nc.vector.tensor_copy(out=swap[:, c:P:2], in_=ident[:, 1 - c : P : 2])
        ident_bf = keep.tile([P, P], BF16)
        nc.vector.tensor_copy(out=ident_bf[:], in_=ident[:])
        warm = keep.tile([P, 1], F32)
        nc.scalar.activation(out=warm[:], in_=one_col[:], func=ACT.Abs_reciprocal_sqrt)

        grouped = [
            keep.tile([P, PASSES, P, 4], BF16, name="grouped%d" % t, align_bytes=64)
            for t in range(TOKEN_TILES)
        ]
        x_codes = [
            keep.tile([P, PASSES * P], U32, name="x_codes%d" % t, align_bytes=64)
            for t in range(TOKEN_TILES)
        ]
        x_planes = [
            keep.tile([P, PASSES * P], U8, name="x_planes%d" % t, align_bytes=64)
            for t in range(TOKEN_TILES)
        ]

        def transpose_tokens(t):
            x_words = x_sb[:, t, :].bitcast(F32)
            banks = []
            for gp in range(PASSES):
                flipped = psum_short.tile([P, 2, P], F32, name="short")
                for u in range(2):
                    first = gp * (K_PASS // 2) + u
                    nc.tensor.transpose(
                        flipped[:, u, :], x_words[:, first : (gp + 1) * (K_PASS // 2) : 2], ident[:]
                    )
                banks.append(flipped)
            return banks

        def regroup_tokens(t, banks):
            copy_of_pass = (nc.scalar.copy, nc.vector.tensor_copy if t == FIRST else nc.scalar.copy)
            for gp, copy in enumerate(copy_of_pass):
                copy(
                    out=grouped[t][:, gp, :, :].rearrange("p s v -> p (s v)").bitcast(F32)
                    .rearrange("p (s u) -> p s u", u=2),
                    in_=banks[gp][:].rearrange("p u s -> p s u"),
                )

        def quantise_tokens(t, passes):
            words = slice(passes.start * P, passes.stop * P)
            nc.vector.quantize_mx(
                out=x_codes[t][:, words].bitcast(FP8X4),
                scales=x_planes[t][:, words],
                in_=grouped[t][:, passes, :, :].rearrange("p g s v -> p (g s v)"),
            )

        columns = keep.tile([P, HEADS], F32)
        gain = keep.tile([P, 1], F32)
        bias_all = keep.tile([P, FEATURES], BF16)

        def spread_bias(c):
            everywhere = psum_short.tile([P, BANK], BF16, name="short")
            for hh in range(CHUNK_HEADS):
                h = c * CHUNK_HEADS + hh
                nc.tensor.matmul(
                    everywhere[:, hh * HEAD : (hh + 1) * HEAD],
                    lhsT=ident_bf[:, h : h + 1].to_broadcast([P, P]), rhs=b_rows[:],
                    start=True, stop=True,
                )
            return everywhere

        def keep_bias(copy, c, everywhere):
            copy(out=bias_all[:, c * BANK : (c + 1) * BANK], in_=everywhere[:])

        tables = keep.tile([P, TOKEN_TILES, 2, HEAD], BF16)

        def regroup_tables():
            quads = freq_sb[:].rearrange("p t (j q) -> p t j q", q=4)
            for which, view in enumerate((quads[:, :, :, 0:4:3], quads[:, :, :, 2:0:-1])):
                nc.vector.tensor_copy(
                    out=tables[:, :, which, :].rearrange("p t (j c) -> p t j c", c=2), in_=view
                )

        table_flipped = keep.tile([P, TOKEN_TILES, 2, P], F32)

        def flip_small():
            small = psum_short.tile([P, 6, P], BF16, name="short")
            nc.tensor.transpose(small[:, 4, :], b_rows[:], ident_bf[:])
            for t in range(TOKEN_TILES):
                for which in range(2):
                    nc.tensor.transpose(small[:, 2 * t + which, :], tables[:, t, which, :], ident_bf[:])
            nc.tensor.transpose(small[:, 5, :], g_row[:], ident_bf[:])
            return small

        def keep_columns(small):
            nc.scalar.copy(out=gain[:], in_=small[:, 5, 0:1])
            nc.scalar.copy(out=columns[:], in_=small[:, 4, 0:HEADS])

        def keep_flipped_table(t, flipped):
            nc.scalar.activation(
                out=table_flipped[:, t, :, :], in_=flipped[:, 2 * t : 2 * t + 2, :], func=ACT.Copy,
                scale=gain[:],
            )

        table_psum = psum_table.tile([P, 2, HEAD], F32, name="table_psum")
        table_sbuf = keep.tile([P, HEAD], F32)

        def flip_table_back():
            for which, order in enumerate((ident, swap)):
                nc.tensor.transpose(table_psum[:, which, :], table_flipped[:, SECOND, which, :], order[:])

        def keep_table_for_gpsimd():
            nc.scalar.copy(out=table_sbuf[:], in_=table_psum[:, 0, :])

        def project(c):
            acc = psum_acc.tile([P, BANK], F32, name="acc")
            for gp in range(PASSES):
                nc.tensor.matmul_mx(
                    out=acc[:],
                    lhsT=x_codes[SECOND][:, gp * P : (gp + 1) * P].bitcast(FP8X4),
                    lhsT_scale=x_planes[SECOND][:, gp * P : (gp + 1) * P],
                    rhs=w_sb[c][:, gp, :].bitcast(FP4X4),
                    rhs_scale=w_planes[:, gp, c * BANK : (c + 1) * BANK],
                    start=(gp == 0),
                    stop=(gp == PASSES - 1),
                )
            return acc

        def project_flipped(piece):
            flipped = psum_short.tile([P, PIECE_HEADS, P], F32, name="short")
            for i in range(PIECE_HEADS):
                h = piece * PIECE_HEADS + i
                hh = h % CHUNK_HEADS
                for gp in range(PASSES):
                    nc.tensor.matmul_mx(
                        out=flipped[:, i, :],
                        lhsT=w_sb[h // CHUNK_HEADS][:, gp, 2 * hh * HEAD : 2 * (hh + 1) * HEAD].bitcast(FP4X4),
                        lhsT_scale=w_planes[:, gp, h * HEAD : (h + 1) * HEAD],
                        rhs=x_codes[FIRST][:, gp * P : (gp + 1) * P].bitcast(FP8X4),
                        rhs_scale=x_planes[FIRST][:, gp * P : (gp + 1) * P],
                        start=(gp == 0),
                        stop=(gp == PASSES - 1),
                    )
            return flipped

        flipped_squares = keep.tile([P, HEADS, P], F32)
        flipped_parts = keep.tile([P, HEADS, 2, P], F32)

        def square_flipped(piece, flipped):
            for i in range(PIECE_HEADS):
                h = piece * PIECE_HEADS + i
                nc.scalar.activation(
                    out=flipped_squares[:, h, :], in_=flipped[:, i, :], func=ACT.Square,
                    bias=columns[:, h : h + 1],
                )

        def multiply_flipped(piece, flipped):
            for i in range(PIECE_HEADS):
                h = piece * PIECE_HEADS + i
                nc.vector.scalar_tensor_tensor(
                    out=flipped_parts[:, h, :, :],
                    in0=flipped[:, i, :].unsqueeze(1).to_broadcast([P, 2, P]),
                    scalar=columns[:, h : h + 1],
                    in1=table_flipped[:, FIRST, :, :],
                    op0=ALU.add,
                    op1=ALU.mult,
                )

        def sum_squares_flipped(c):
            sums_bank = psum_short.tile([P, CHUNK_HEADS], F32, name="short")
            for hh in range(CHUNK_HEADS):
                nc.tensor.matmul(
                    sums_bank[:, hh : hh + 1], lhsT=flipped_squares[:, c * CHUNK_HEADS + hh, :],
                    rhs=one_col[:], start=True, stop=True,
                )
            return sums_bank

        def flip_parts_back(heads, values):
            for h in heads:
                for which, order in enumerate((ident, swap)):
                    nc.tensor.matmul(
                        values[:, (h - heads.start) * HEAD : (h - heads.start + 1) * HEAD],
                        lhsT=flipped_parts[:, h, which, :], rhs=order[:],
                        is_transpose=True, start=(which == 0), stop=(which == 1),
                    )

        u = keep.tile([P, FEATURES], F32)
        squares = keep.tile([P, FEATURES], F32)
        sums = keep.tile([P, HEADS], F32)
        rstd = [keep.tile([P, HEADS], F32, name="rstd%d" % t) for t in range(TOKEN_TILES)]
        parts = [keep.tile([P, FEATURES], F32, name="part%d" % cc) for cc in range(2)]
        rotated = keep.tile([P, FEATURES], F32)
        result = [keep.tile([P, FEATURES], F32, name="result%d" % t) for t in range(TOKEN_TILES)]

        def add_bias(c, acc):
            nc.vector.tensor_tensor(
                out=u[:, c * BANK : (c + 1) * BANK], in0=acc[:], in1=bias_all[:, c * BANK : (c + 1) * BANK],
                op=ALU.add,
            )

        def square_sums(c):
            for hh in range(CHUNK_HEADS):
                h = c * CHUNK_HEADS + hh
                nc.scalar.activation(
                    out=squares[:, h * HEAD : (h + 1) * HEAD],
                    in_=u[:, h * HEAD : (h + 1) * HEAD],
                    func=ACT.Square,
                    accum_out=sums[:, h : h + 1],
                )

        def norm_factor(t, heads, source):
            nc.scalar.activation(
                out=rstd[t][:, heads], in_=source[:], func=ACT.Abs_reciprocal_sqrt,
                scale=1.0 / HEAD, bias=EPS,
            )

        def multiply(engine, pieces, which, in_psum=True):
            cols = slice(pieces.start * PIECE, pieces.stop * PIECE)
            heads = len(pieces) * PIECE_HEADS
            values = u[:, cols].rearrange("p (h j c) -> p h j c", h=heads, c=2)
            factors = table_psum[:, which, :] if in_psum else table_sbuf[:]
            engine.tensor_tensor(
                out=parts[which][:, cols].rearrange("p (h j i) -> p h j i", h=heads, i=2),
                in0=values[:, :, :, ::-1] if which else values,
                in1=factors.rearrange("p (j i) -> p j i", i=2).unsqueeze(1)
                .to_broadcast([P, heads, PAIRS, 2]),
                op=ALU.mult,
            )

        def add_products(engine, cols):
            engine.tensor_tensor(
                out=rotated[:, cols], in0=parts[0][:, cols], in1=parts[1][:, cols], op=ALU.add,
            )

        def scale_and_store(t, piece, source, offset):
            for h in range(piece * PIECE_HEADS, (piece + 1) * PIECE_HEADS):
                nc.scalar.activation(
                    out=result[t][:, h * HEAD : (h + 1) * HEAD],
                    in_=source[:, h * HEAD - offset : (h + 1) * HEAD - offset],
                    func=ACT.Copy,
                    scale=rstd[t][:, h : h + 1],
                )
            cols = slice(piece * PIECE, (piece + 1) * PIECE)
            nc.sync.dma_start(out=out_rows[t * P : (t + 1) * P, cols], in_=result[t][:, cols])

        def scale_and_store_by(engine, t, piece, source, offset):
            cols = slice(piece * PIECE, (piece + 1) * PIECE)
            engine.tensor_tensor(
                out=result[t][:, cols].rearrange("p (h d) -> p h d", d=HEAD),
                in0=source[:, cols.start - offset : cols.stop - offset]
                .rearrange("p (h d) -> p h d", d=HEAD),
                in1=rstd[t][:, piece * PIECE_HEADS : (piece + 1) * PIECE_HEADS]
                .unsqueeze(2).to_broadcast([P, PIECE_HEADS, HEAD]),
                op=ALU.mult,
            )
            nc.sync.dma_start(out=out_rows[t * P : (t + 1) * P, cols], in_=result[t][:, cols])

        banks_of = [transpose_tokens(t) for t in range(TOKEN_TILES)]
        regroup_tables()
        regroup_tokens(FIRST, banks_of[FIRST])
        for gp in range(PASSES):
            quantise_tokens(FIRST, slice(gp, gp + 1))
        everywhere = [spread_bias(0)]
        regroup_tokens(SECOND, banks_of[SECOND])
        quantise_tokens(SECOND, slice(0, PASSES))
        keep_bias(nc.vector.tensor_copy, 0, everywhere[0])
        small = flip_small()
        keep_columns(small)
        for t in range(TOKEN_TILES):
            keep_flipped_table(t, small)
        flipped = [project_flipped(piece) for piece in range(2)]
        acc = [project(0)]
        flip_table_back()
        everywhere.append(spread_bias(1))
        acc.append(project(1))
        square_flipped(1, flipped[1])
        multiply_flipped(0, flipped[0])
        square_flipped(0, flipped[0])
        add_bias(0, acc[0])
        keep_table_for_gpsimd()
        keep_bias(nc.scalar.copy, 1, everywhere[1])
        multiply(nc.gpsimd, range(2), 0, in_psum=False)
        multiply_flipped(1, flipped[1])
        multiply(nc.vector, range(2), 1)
        add_products(nc.gpsimd, slice(0, BANK))
        add_bias(1, acc[1])
        square_sums(0)
        flipped += [project_flipped(piece) for piece in range(2, 4)]
        sums_of = [sum_squares_flipped(0)]
        values = psum_short.tile([P, BANK], F32, name="short")
        flip_parts_back(range(0, CHUNK_HEADS), values)
        for which in range(2):
            multiply(nc.vector, range(2, 3), which)
        add_products(nc.gpsimd, slice(2 * PIECE, 3 * PIECE))
        for piece in range(2, 4):
            square_flipped(piece, flipped[piece])
            multiply_flipped(piece, flipped[piece])
        for which in range(2):
            multiply(nc.vector, range(3, 4), which)
        sums_of.append(sum_squares_flipped(1))
        norm_factor(FIRST, slice(0, CHUNK_HEADS), sums_of[0])
        square_sums(1)
        scale_and_store(FIRST, 0, values, 0)
        scale_and_store(FIRST, 1, values, 0)
        norm_factor(SECOND, slice(0, HEADS), sums)
        scale_and_store(SECOND, 0, rotated, 0)
        norm_factor(FIRST, slice(CHUNK_HEADS, HEADS), sums_of[1])
        scale_and_store(SECOND, 1, rotated, 0)
        add_products(nc.vector, slice(3 * PIECE, 4 * PIECE))
        values = []
        for piece in range(2, 4):
            bank = psum_acc.tile([P, BANK], F32, name="acc")
            flip_parts_back(range(piece * PIECE_HEADS, (piece + 1) * PIECE_HEADS), bank)
            values.append(bank)
        scale_and_store(FIRST, 2, values[0], 2 * PIECE)
        scale_and_store(SECOND, 2, rotated, 0)
        scale_and_store_by(nc.vector, FIRST, 3, values[1], 3 * PIECE)
        scale_and_store(SECOND, 3, rotated, 0)
